import numpy as np
import ml_dtypes


def mxq(x, axis, fmt="e4m3"):
    dtype, down = {"e4m3": (ml_dtypes.float8_e4m3fn, 7), "e5m2": (ml_dtypes.float8_e5m2, 14)}[fmt]
    v = np.moveaxis(np.asarray(x, np.float32).astype(ml_dtypes.bfloat16).astype(np.float64), axis, -1)
    blocks = v.reshape(v.shape[:-1] + (-1, 32))
    amax = np.abs(blocks).max(-1, keepdims=True)
    byte = np.maximum(np.where(amax > 0, np.frexp(amax)[1] - 1 + 127, 0) - down, 1)
    scale = np.exp2(byte - 127.0)
    codes = (blocks / scale).astype(np.float32).astype(dtype).astype(np.float64)
    return np.moveaxis((codes * scale).reshape(v.shape), -1, axis)


WIDE = False


def mx_kscale(k):
    if not WIDE:
        return np.ones(k)
    levels = np.array([10, -10, 5, -5, 0])
    a = np.random.permutation(np.resize(levels, k // 512 * 4)).reshape(k // 512, 4)
    idx = np.arange(k)
    return np.exp2(a[idx // 512, idx % 128 // 32])


BF16 = ml_dtypes.bfloat16


def bf(x):
    return np.asarray(x, np.float32).astype(BF16)


def f64(x):
    return np.asarray(x).astype(np.float64)


E2M1 = np.array([0.0, 0.5, 1.0, 1.5, 2.0, 3.0, 4.0, 6.0, -0.0, -0.5, -1.0, -1.5, -2.0, -3.0, -4.0, -6.0])


def pack_weight(w, fmt):
    k, n = w.shape
    w = f64(bf(w)).reshape(k // 32, 32, n)
    amax = np.abs(w).max(1)
    if fmt == "e4m3":
        byte = np.frexp(amax)[1] - 1 + 127 - 7
    else:
        mant, ex = np.frexp(amax / 6.0)
        byte = np.where(mant > 0.5, ex, ex - 1) + 127
    byte = np.clip(np.where(amax > 0, byte, 1), 1, 254)
    scaled = (w * np.exp2(127.0 - byte)[:, None, :]).reshape(k, n).astype(np.float32)
    by_word = np.ascontiguousarray(scaled.reshape(k // 512, 128, 4, n).transpose(0, 1, 3, 2))
    if fmt == "e4m3":
        words = by_word.astype(ml_dtypes.float8_e4m3fn).view(np.uint8)
    else:
        c = by_word.astype(ml_dtypes.float4_e2m1fn).view(np.uint8) & 0xF
        words = c[..., 0::2] | (c[..., 1::2] << 4)
    return np.ascontiguousarray(words), np.ascontiguousarray(byte.astype(np.uint8).reshape(k // 512, 16, n))


def unpack_weight(words, scales, fmt):
    g, p, n, _ = words.shape
    if fmt == "e4m3":
        vals = np.ascontiguousarray(words).view(ml_dtypes.float8_e4m3fn).astype(np.float64)
    else:
        nib = np.empty((g, p, n, 4), np.uint8)
        nib[..., 0::2] = words & 0xF
        nib[..., 1::2] = words >> 4
        vals = E2M1[nib]
    vals = vals * np.repeat(np.exp2(scales.astype(np.float64) - 127.0), 8, axis=1)[..., None]
    return vals.transpose(0, 1, 3, 2).reshape(g * 512, n)


B, C, CQ, CV, H, W = 2, 1024, 128, 1024, 32, 64
P = H * W
FMT = "e4m3"


def conv1x1(xq, w_words, w_scales, b):
    wt = unpack_weight(w_words, w_scales, FMT)
    y = (wt.T @ xq) + f64(b)[None, :, None]
    return y.reshape(B, wt.shape[1], H, W)


def kronecker(y):
    return np.concatenate([y.mean(axis=3), y.mean(axis=2)], axis=2)


def setup_inputs():
    s = mx_kscale(C)
    g = 3.0 / np.sqrt(C)
    x = bf(np.random.standard_normal((B, C, H, W)) * s[None, :, None, None])
    Wq_words, Wq_scales = pack_weight(np.ascontiguousarray((np.random.standard_normal((CQ, C)) * g / s[None, :]).T), FMT)
    bq = bf(np.random.standard_normal(CQ) * 0.1)
    Wk_words, Wk_scales = pack_weight(np.ascontiguousarray((np.random.standard_normal((CQ, C)) * g / s[None, :]).T), FMT)
    bk = bf(np.random.standard_normal(CQ) * 0.1)
    Wv_words, Wv_scales = pack_weight(np.ascontiguousarray((np.random.standard_normal((CV, C)) * g / s[None, :]).T), FMT)
    bv = bf(np.random.standard_normal(CV) * 0.1)
    return {"x": x,
            "Wq_words": Wq_words, "Wq_scales": Wq_scales,
            "bq": bq,
            "Wk_words": Wk_words, "Wk_scales": Wk_scales,
            "bk": bk,
            "Wv_words": Wv_words, "Wv_scales": Wv_scales,
            "bv": bv}


def reference(x, Wq_words, Wq_scales, bq, Wk_words, Wk_scales, bk, Wv_words, Wv_scales, bv):
    xq = mxq(f64(x).reshape(B, C, P), 1, "e4m3")
    q = kronecker(conv1x1(xq, Wq_words, Wq_scales, bq))
    k = kronecker(conv1x1(xq, Wk_words, Wk_scales, bk))
    v = kronecker(conv1x1(xq, Wv_words, Wv_scales, bv))
    return q, k, v

@@ -1,0 +1,206 @@
+from contextlib import ExitStack
+
+import concourse.mybir as mybir
+from concourse.masks import make_identity
+
+F32 = mybir.dt.float32
+BF16 = mybir.dt.bfloat16
+U8 = mybir.dt.uint8
+U32 = mybir.dt.uint32
+I32 = mybir.dt.int32
+FP8X4 = mybir.dt.float8_e4m3fn_x4
+ADD = mybir.AluOpType.add
+MULT = mybir.AluOpType.mult
+AXIS_X = mybir.AxisListType.X
+COPY = mybir.ActivationFunctionType.Copy
+
+P = 128
+PACK = 4
+K_PASS = P * PACK
+BATCH, CHANNELS, HEIGHT, WIDTH = 2, 1024, 32, 64
+PASSES = CHANNELS // K_PASS
+PIXELS = HEIGHT * WIDTH
+CHUNK = 512
+ROWS = CHUNK // WIDTH
+CHUNKS = PIXELS // CHUNK
+OUT_Q, OUT_K, OUT_V = 128, 128, 1024
+OUT_ALL = OUT_Q + OUT_K + OUT_V
+TILES = OUT_ALL // P
+
+TENSOR_GROUP = 3
+SHARED_GROUP = 5
+VECTOR_GROUP = TILES - TENSOR_GROUP - SHARED_GROUP
+
+FLOPS = 2 * OUT_ALL * CHANNELS * BATCH * PIXELS
+
+
+def tile_pam_module_pa_kernel(
+    tc, x, Wq_words, Wq_scales, bq, Wk_words, Wk_scales, bk, Wv_words, Wv_scales, bv, out_0, out_1, out_2
+):
+    nc = tc.nc
+    tensor_tiles = list(range(TENSOR_GROUP))
+    shared_tiles = list(range(TENSOR_GROUP, TENSOR_GROUP + SHARED_GROUP))
+    vector_tiles = list(range(TENSOR_GROUP + SHARED_GROUP, TILES))
+    groups = [tensor_tiles, shared_tiles, vector_tiles]
+    tile_order = [group[r] for r in range(TILES) for group in groups if r < len(group)]
+
+    with ExitStack() as ctx:
+        keep = ctx.enter_context(tc.tile_pool(name="keep", bufs=1))
+        stage = ctx.enter_context(tc.tile_pool(name="stage", bufs=4))
+        products = ctx.enter_context(tc.tile_pool(name="products", bufs=8))
+        banks = ctx.enter_context(tc.psum_pool(name="banks", bufs=8 - TENSOR_GROUP))
+        column_banks = ctx.enter_context(tc.psum_pool(name="column_banks", bufs=TENSOR_GROUP))
+
+        x_view = x.rearrange("n (g p t) h w -> n g p t (h w)", g=PASSES, p=P, t=PACK)
+        raw = {}
+
+        def load_chunk(c):
+            n, part = divmod(c, CHUNKS)
+            for g in range(PASSES):
+                raw[c, g] = keep.tile([P, PACK, CHUNK], BF16, name="raw%d_%d" % (c, g))
+                nc.sync.dma_start(out=raw[c, g][:], in_=x_view[n, g, :, :, CHUNK * part : CHUNK * (part + 1)])
+
+        load_chunk(0)
+
+        w_codes = keep.tile([P, PASSES, OUT_ALL], U32, align_bytes=64)
+        w_scales = keep.tile([P, PASSES, OUT_ALL], U8, align_bytes=64)
+        nc.vector.memset(w_scales[:].bitcast(I32), 0)
+        first = 0
+        for words, scales, width in ((Wq_words, Wq_scales, OUT_Q), (Wk_words, Wk_scales, OUT_K), (Wv_words, Wv_scales, OUT_V)):
+            cols = slice(first, first + width)
+            first += width
+            scale_rows = scales.rearrange("g q n -> q g n")
+            for quadrant in range(4):
+                nc.sync.dma_start(
+                    out=w_scales[32 * quadrant : 32 * quadrant + 4, :, cols].bitcast(I32),
+                    in_=scale_rows[4 * quadrant : 4 * quadrant + 4].bitcast(I32),
+                )
+            nc.sync.dma_start(
+                out=w_codes[:, :, cols].bitcast(I32),
+                in_=words.rearrange("g p n t -> p g (n t)").bitcast(I32),
+            )
+
+        load_chunk(1)
+
+        bias_rows = keep.tile([P, P], BF16)
+        nc.gpsimd.memset(bias_rows[:], 0.0)
+        nc.sync.dma_start(out=bias_rows[0:1, :], in_=bq.rearrange("(m p) -> m p", p=P))
+        nc.sync.dma_start(out=bias_rows[1:2, :], in_=bk.rearrange("(m p) -> m p", p=P))
+        nc.sync.dma_start(out=bias_rows[2:TILES, :], in_=bv.rearrange("(m p) -> m p", p=P))
+        identity = keep.tile([P, P], BF16)
+        make_identity(nc, identity[:])
+
+        for c in range(2, BATCH * CHUNKS):
+            load_chunk(c)
+
+        x_codes = {}
+        x_scales = {}
+
+        def quantise_chunk(c):
+            x_codes[c] = keep.tile([P, PASSES, CHUNK], U32, name="x_codes%d" % c, align_bytes=64)
+            x_scales[c] = keep.tile([P, PASSES, CHUNK], U8, name="x_scales%d" % c, align_bytes=64)
+            for g in range(PASSES):
+                grouped = stage.tile([P, CHUNK, PACK], BF16, align_bytes=64)
+                by_pixel = raw[c, g][:].rearrange("p t w -> p w t")
+                if c == 0:
+                    nc.vector.tensor_copy(out=grouped[:], in_=by_pixel)
+                else:
+                    nc.gpsimd.tensor_scalar(out=grouped[:], in0=by_pixel, scalar1=1.0, scalar2=0.0, op0=MULT, op1=ADD)
+                nc.vector.quantize_mx(
+                    out=x_codes[c][:, g, :].bitcast(FP8X4),
+                    scales=x_scales[c][:, g, :],
+                    in_=grouped[:].rearrange("p w t -> p (w t)"),
+                )
+
+        row_sum = keep.tile([P, BATCH, TILES, HEIGHT], F32)
+        col_part = keep.tile([P, BATCH, TILES, CHUNKS, WIDTH], F32)
+        col_sum = keep.tile([P, BATCH, TILES, WIDTH], F32)
+        pooled = keep.tile([P, BATCH, TILES, HEIGHT + WIDTH], F32)
+        bias = keep.tile([P, TILES], F32)
+        column_bank = {}
+
+        def multiply(bank, c, m, start, stop):
+            for g in range(PASSES):
+                nc.tensor.matmul_mx(
+                    out=bank[:],
+                    lhsT=w_codes[:, g, P * m : P * (m + 1)].bitcast(FP8X4),
+                    lhsT_scale=w_scales[:, g, P * m : P * (m + 1)],
+                    rhs=x_codes[c][:, g, :].bitcast(FP8X4),
+                    rhs_scale=x_scales[c][:, g, :],
+                    start=start and g == 0,
+                    stop=stop and g == PASSES - 1,
+                )
+
+        def convolve_chunk(c):
+            n, part = divmod(c, CHUNKS)
+            for m in tile_order:
+                bank = banks.tile([P, CHUNK], F32, tag="bank")
+                multiply(bank, c, m, True, True)
+                rows = slice(ROWS * part, ROWS * (part + 1))
+                if m in vector_tiles:
+                    nc.vector.tensor_reduce(
+                        out=row_sum[:, n, m, rows], in_=bank[:].rearrange("p (i j) -> p i j", j=WIDTH), axis=AXIS_X, op=ADD
+                    )
+                    nc.vector.tensor_reduce(
+                        out=col_part[:, n, m, part, :], in_=bank[:].rearrange("p (i j) -> p j i", j=WIDTH), axis=AXIS_X, op=ADD
+                    )
+                    continue
+                product = products.tile([P, ROWS, WIDTH], F32)
+                for i in range(ROWS):
+                    nc.scalar.activation(
+                        out=product[:, i, :],
+                        in_=bank[:, WIDTH * i : WIDTH * (i + 1)],
+                        func=COPY,
+                        accum_out=row_sum[:, n, m, ROWS * part + i : ROWS * part + i + 1],
+                    )
+                if m in shared_tiles:
+                    nc.vector.tensor_reduce(
+                        out=col_part[:, n, m, part, :], in_=product[:].rearrange("p i j -> p j i"), axis=AXIS_X, op=ADD
+                    )
+                else:
+                    if part == 0:
+                        column_bank[m] = column_banks.tile([P, CHUNK], F32, tag="column_bank", name="column_bank%d_%d" % (n, m))
+                    multiply(column_bank[m], c, m, part == 0, part == CHUNKS - 1)
+
+        def finish_map(n):
+            for m in tensor_tiles:
+                nc.vector.tensor_reduce(
+                    out=col_sum[:, n, m, :], in_=column_bank[m][:].rearrange("p (i j) -> p j i", j=WIDTH), axis=AXIS_X, op=ADD
+                )
+            nc.vector.tensor_reduce(
+                out=col_sum[:, n, TENSOR_GROUP:, :],
+                in_=col_part[:, n, TENSOR_GROUP:, :, :].rearrange("p m c j -> p m j c"),
+                axis=AXIS_X,
+                op=ADD,
+            )
+            nc.vector.scalar_tensor_tensor(
+                out=pooled[:, n, :, 0:HEIGHT],
+                in0=row_sum[:, n, :, :],
+                scalar=1.0 / WIDTH,
+                in1=bias[:].unsqueeze(2).to_broadcast([P, TILES, HEIGHT]),
+                op0=MULT,
+                op1=ADD,
+            )
+            nc.vector.scalar_tensor_tensor(
+                out=pooled[:, n, :, HEIGHT:],
+                in0=col_sum[:, n, :, :],
+                scalar=1.0 / HEIGHT,
+                in1=bias[:].unsqueeze(2).to_broadcast([P, TILES, WIDTH]),
+                op0=MULT,
+                op1=ADD,
+            )
+            nc.sync.dma_start(out=out_0[n], in_=pooled[:, n, 0, :])
+            nc.sync.dma_start(out=out_1[n], in_=pooled[:, n, 1, :])
+            nc.sync.dma_start(out=out_2[n].rearrange("(m p) f -> p m f", p=P), in_=pooled[:, n, 2:, :])
+
+        quantise_chunk(0)
+        for c in range(BATCH * CHUNKS):
+            if c + 1 < BATCH * CHUNKS:
+                quantise_chunk(c + 1)
+            convolve_chunk(c)
+            if c == 0:
+                bias_bank = banks.tile([P, P], BF16, tag="bank")
+                nc.tensor.transpose(bias_bank[:], bias_rows[:], identity[:])
+                nc.vector.tensor_copy(out=bias[:], in_=bias_bank[:, 0:TILES])
+            if c % CHUNKS == CHUNKS - 1:
+                finish_map(c // CHUNKS)

@@ -23,13 +23,18 @@ PIXELS = HEIGHT * WIDTH
 CHUNK = 512
 ROWS = CHUNK // WIDTH
 CHUNKS = PIXELS // CHUNK
+ALL_CHUNKS = BATCH * CHUNKS
 OUT_Q, OUT_K, OUT_V = 128, 128, 1024
 OUT_ALL = OUT_Q + OUT_K + OUT_V
 TILES = OUT_ALL // P
+PSUM_BANKS = 8
 
 TENSOR_GROUP = 3
-SHARED_GROUP = 5
+SHARED_GROUP = 4
 VECTOR_GROUP = TILES - TENSOR_GROUP - SHARED_GROUP
+
+QUANTISE_AT = 6
+FINISH_AT = 3
 
 FLOPS = 2 * OUT_ALL * CHANNELS * BATCH * PIXELS
 
@@ -47,9 +52,10 @@ def tile_pam_module_pa_kernel(
     with ExitStack() as ctx:
         keep = ctx.enter_context(tc.tile_pool(name="keep", bufs=1))
         stage = ctx.enter_context(tc.tile_pool(name="stage", bufs=4))
-        products = ctx.enter_context(tc.tile_pool(name="products", bufs=8))
-        banks = ctx.enter_context(tc.psum_pool(name="banks", bufs=8 - TENSOR_GROUP))
+        products = ctx.enter_context(tc.tile_pool(name="products", bufs=4))
+        banks = ctx.enter_context(tc.psum_pool(name="banks", bufs=PSUM_BANKS - TENSOR_GROUP))
         column_banks = ctx.enter_context(tc.psum_pool(name="column_banks", bufs=TENSOR_GROUP))
+        ctx.enter_context(tc.manual_schedule())
 
         x_view = x.rearrange("n (g p t) h w -> n g p t (h w)", g=PASSES, p=P, t=PACK)
         raw = {}
@@ -65,22 +71,22 @@ def tile_pam_module_pa_kernel(
         w_codes = keep.tile([P, PASSES, OUT_ALL], U32, align_bytes=64)
         w_scales = keep.tile([P, PASSES, OUT_ALL], U8, align_bytes=64)
         nc.vector.memset(w_scales[:].bitcast(I32), 0)
-        first = 0
-        for words, scales, width in ((Wq_words, Wq_scales, OUT_Q), (Wk_words, Wk_scales, OUT_K), (Wv_words, Wv_scales, OUT_V)):
-            cols = slice(first, first + width)
-            first += width
+        weights = ((Wq_words, Wq_scales, 0, OUT_Q), (Wk_words, Wk_scales, OUT_Q, OUT_K), (Wv_words, Wv_scales, OUT_Q + OUT_K, OUT_V))
+        for words, scales, first, width in weights:
+            nc.sync.dma_start(
+                out=w_codes[:, :, first : first + width].bitcast(I32),
+                in_=words.rearrange("g p n t -> p g (n t)").bitcast(I32),
+            )
+        for words, scales, first, width in weights:
             scale_rows = scales.rearrange("g q n -> q g n")
             for quadrant in range(4):
                 nc.sync.dma_start(
-                    out=w_scales[32 * quadrant : 32 * quadrant + 4, :, cols].bitcast(I32),
+                    out=w_scales[32 * quadrant : 32 * quadrant + 4, :, first : first + width].bitcast(I32),
                     in_=scale_rows[4 * quadrant : 4 * quadrant + 4].bitcast(I32),
                 )
-            nc.sync.dma_start(
-                out=w_codes[:, :, cols].bitcast(I32),
-                in_=words.rearrange("g p n t -> p g (n t)").bitcast(I32),
-            )
 
         load_chunk(1)
+        load_chunk(2)
 
         bias_rows = keep.tile([P, P], BF16)
         nc.gpsimd.memset(bias_rows[:], 0.0)
@@ -90,26 +96,39 @@ def tile_pam_module_pa_kernel(
         identity = keep.tile([P, P], BF16)
         make_identity(nc, identity[:])
 
-        for c in range(2, BATCH * CHUNKS):
+        for c in range(3, ALL_CHUNKS):
             load_chunk(c)
 
+        grouped = {}
         x_codes = {}
         x_scales = {}
+
+        def regroup_chunk(c):
+            for g in range(PASSES):
+                grouped[c, g] = stage.tile([P, CHUNK, PACK], BF16, tag="grouped", name="grouped%d_%d" % (c, g), align_bytes=64)
+                if c == 0:
+                    nc.vector.tensor_copy(
+                        out=grouped[c, g][:].rearrange("p (w i) t -> p w t i", i=4),
+                        in_=raw[c, g][:].rearrange("p t (w i) -> p w t i", i=4),
+                    )
+                else:
+                    nc.gpsimd.tensor_scalar(
+                        out=grouped[c, g][:],
+                        in0=raw[c, g][:].rearrange("p t w -> p w t"),
+                        scalar1=1.0,
+                        scalar2=0.0,
+                        op0=MULT,
+                        op1=ADD,
+                    )
 
         def quantise_chunk(c):
             x_codes[c] = keep.tile([P, PASSES, CHUNK], U32, name="x_codes%d" % c, align_bytes=64)
             x_scales[c] = keep.tile([P, PASSES, CHUNK], U8, name="x_scales%d" % c, align_bytes=64)
             for g in range(PASSES):
-                grouped = stage.tile([P, CHUNK, PACK], BF16, align_bytes=64)
-                by_pixel = raw[c, g][:].rearrange("p t w -> p w t")
-                if c == 0:
-                    nc.vector.tensor_copy(out=grouped[:], in_=by_pixel)
-                else:
-                    nc.gpsimd.tensor_scalar(out=grouped[:], in0=by_pixel, scalar1=1.0, scalar2=0.0, op0=MULT, op1=ADD)
                 nc.vector.quantize_mx(
                     out=x_codes[c][:, g, :].bitcast(FP8X4),
                     scales=x_scales[c][:, g, :],
-                    in_=grouped[:].rearrange("p w t -> p (w t)"),
+                    in_=grouped[c, g][:].rearrange("p w t -> p (w t)"),
                 )
 
         row_sum = keep.tile([P, BATCH, TILES, HEIGHT], F32)
@@ -131,42 +150,10 @@ def tile_pam_module_pa_kernel(
                     stop=stop and g == PASSES - 1,
                 )
 
-        def convolve_chunk(c):
-            n, part = divmod(c, CHUNKS)
-            for m in tile_order:
-                bank = banks.tile([P, CHUNK], F32, tag="bank")
-                multiply(bank, c, m, True, True)
-                rows = slice(ROWS * part, ROWS * (part + 1))
-                if m in vector_tiles:
-                    nc.vector.tensor_reduce(
-                        out=row_sum[:, n, m, rows], in_=bank[:].rearrange("p (i j) -> p i j", j=WIDTH), axis=AXIS_X, op=ADD
-                    )
-                    nc.vector.tensor_reduce(
-                        out=col_part[:, n, m, part, :], in_=bank[:].rearrange("p (i j) -> p j i", j=WIDTH), axis=AXIS_X, op=ADD
-                    )
-                    continue
-                product = products.tile([P, ROWS, WIDTH], F32)
-                for i in range(ROWS):
-                    nc.scalar.activation(
-                        out=product[:, i, :],
-                        in_=bank[:, WIDTH * i : WIDTH * (i + 1)],
-                        func=COPY,
-                        accum_out=row_sum[:, n, m, ROWS * part + i : ROWS * part + i + 1],
-                    )
-                if m in shared_tiles:
-                    nc.vector.tensor_reduce(
-                        out=col_part[:, n, m, part, :], in_=product[:].rearrange("p i j -> p j i"), axis=AXIS_X, op=ADD
-                    )
-                else:
-                    if part == 0:
-                        column_bank[m] = column_banks.tile([P, CHUNK], F32, tag="column_bank", name="column_bank%d_%d" % (n, m))
-                    multiply(column_bank[m], c, m, part == 0, part == CHUNKS - 1)
+        def sum_over_rows(out, eight_rows):
+            nc.vector.tensor_reduce(out=out, in_=eight_rows.rearrange("p i j -> p j i"), axis=AXIS_X, op=ADD)
 
         def finish_map(n):
-            for m in tensor_tiles:
-                nc.vector.tensor_reduce(
-                    out=col_sum[:, n, m, :], in_=column_bank[m][:].rearrange("p (i j) -> p j i", j=WIDTH), axis=AXIS_X, op=ADD
-                )
             nc.vector.tensor_reduce(
                 out=col_sum[:, n, TENSOR_GROUP:, :],
                 in_=col_part[:, n, TENSOR_GROUP:, :, :].rearrange("p m c j -> p m j c"),
@@ -193,14 +180,51 @@ def tile_pam_module_pa_kernel(
             nc.sync.dma_start(out=out_1[n], in_=pooled[:, n, 1, :])
             nc.sync.dma_start(out=out_2[n].rearrange("(m p) f -> p m f", p=P), in_=pooled[:, n, 2:, :])
 
+        regroup_chunk(0)
+        regroup_chunk(1)
         quantise_chunk(0)
-        for c in range(BATCH * CHUNKS):
-            if c + 1 < BATCH * CHUNKS:
-                quantise_chunk(c + 1)
-            convolve_chunk(c)
+        copied = []
+        ended = []
+        for c in range(ALL_CHUNKS):
+            n, part = divmod(c, CHUNKS)
+            rows = slice(ROWS * part, ROWS * (part + 1))
+            if c + 2 < ALL_CHUNKS:
+                regroup_chunk(c + 2)
+            for place, m in enumerate(tile_order):
+                if place == QUANTISE_AT and c + 1 < ALL_CHUNKS:
+                    quantise_chunk(c + 1)
+                if place == FINISH_AT and ended:
+                    finish_map(ended.pop())
+                bank = banks.tile([P, CHUNK], F32, tag="bank")
+                multiply(bank, c, m, True, True)
+                by_row = bank[:].rearrange("p (i j) -> p i j", j=WIDTH)
+                if m in vector_tiles:
+                    nc.vector.tensor_reduce(out=row_sum[:, n, m, rows], in_=by_row, axis=AXIS_X, op=ADD)
+                    sum_over_rows(col_part[:, n, m, part, :], by_row)
+                    continue
+                product = products.tile([P, ROWS, WIDTH], F32, tag="product")
+                for i in range(ROWS):
+                    nc.scalar.activation(
+                        out=product[:, i, :],
+                        in_=by_row[:, i, :],
+                        func=COPY,
+                        accum_out=row_sum[:, n, m, ROWS * part + i : ROWS * part + i + 1],
+                    )
+                if m in shared_tiles:
+                    copied.append((col_part[:, n, m, part, :], product[:]))
+                    if len(copied) > 1:
+                        sum_over_rows(*copied.pop(0))
+                else:
+                    if part == 0:
+                        column_bank[m] = column_banks.tile([P, CHUNK], F32, tag="column_bank", name="column_bank%d_%d" % (n, m))
+                    multiply(column_bank[m], c, m, part == 0, part == CHUNKS - 1)
+                    if part == CHUNKS - 1:
+                        sum_over_rows(col_sum[:, n, m, :], column_bank[m][:].rearrange("p (i j) -> p i j", j=WIDTH))
             if c == 0:
                 bias_bank = banks.tile([P, P], BF16, tag="bank")
                 nc.tensor.transpose(bias_bank[:], bias_rows[:], identity[:])
                 nc.vector.tensor_copy(out=bias[:], in_=bias_bank[:, 0:TILES])
-            if c % CHUNKS == CHUNKS - 1:
-                finish_map(c // CHUNKS)
+            if part == CHUNKS - 1:
+                ended.append(n)
+        sum_over_rows(*copied.pop(0))
+        finish_map(ended.pop())

@@ -51,7 +51,7 @@ def tile_pam_module_pa_kernel(
 
     with ExitStack() as ctx:
         keep = ctx.enter_context(tc.tile_pool(name="keep", bufs=1))
-        stage = ctx.enter_context(tc.tile_pool(name="stage", bufs=4))
+        stage = ctx.enter_context(tc.tile_pool(name="stage", bufs=1))
         products = ctx.enter_context(tc.tile_pool(name="products", bufs=4))
         banks = ctx.enter_context(tc.psum_pool(name="banks", bufs=PSUM_BANKS - TENSOR_GROUP))
         column_banks = ctx.enter_context(tc.psum_pool(name="column_banks", bufs=TENSOR_GROUP))
@@ -104,16 +104,16 @@ def tile_pam_module_pa_kernel(
         x_scales = {}
 
         def regroup_chunk(c):
+            grouped[c] = stage.tile([P, PASSES, CHUNK, PACK], BF16, tag="grouped", name="grouped%d" % c, align_bytes=64)
             for g in range(PASSES):
-                grouped[c, g] = stage.tile([P, CHUNK, PACK], BF16, tag="grouped", name="grouped%d_%d" % (c, g), align_bytes=64)
                 if c == 0:
                     nc.vector.tensor_copy(
-                        out=grouped[c, g][:].rearrange("p (w i) t -> p w t i", i=4),
+                        out=grouped[c][:, g].rearrange("p (w i) t -> p w t i", i=4),
                         in_=raw[c, g][:].rearrange("p t (w i) -> p w t i", i=4),
                     )
                 else:
                     nc.gpsimd.tensor_scalar(
-                        out=grouped[c, g][:],
+                        out=grouped[c][:, g],
                         in0=raw[c, g][:].rearrange("p t w -> p w t"),
                         scalar1=1.0,
                         scalar2=0.0,
@@ -124,12 +124,11 @@ def tile_pam_module_pa_kernel(
         def quantise_chunk(c):
             x_codes[c] = keep.tile([P, PASSES, CHUNK], U32, name="x_codes%d" % c, align_bytes=64)
             x_scales[c] = keep.tile([P, PASSES, CHUNK], U8, name="x_scales%d" % c, align_bytes=64)
-            for g in range(PASSES):
-                nc.vector.quantize_mx(
-                    out=x_codes[c][:, g, :].bitcast(FP8X4),
-                    scales=x_scales[c][:, g, :],
-                    in_=grouped[c, g][:].rearrange("p w t -> p (w t)"),
-                )
+            nc.vector.quantize_mx(
+                out=x_codes[c][:].rearrange("p g w -> p (g w)").bitcast(FP8X4),
+                scales=x_scales[c][:].rearrange("p g w -> p (g w)"),
+                in_=grouped[c][:].rearrange("p g w t -> p (g w t)"),
+            )
 
         row_sum = keep.tile([P, BATCH, TILES, HEIGHT], F32)
         col_part = keep.tile([P, BATCH, TILES, CHUNKS, WIDTH], F32)
@@ -181,18 +180,18 @@ def tile_pam_module_pa_kernel(
             nc.sync.dma_start(out=out_2[n].rearrange("(m p) f -> p m f", p=P), in_=pooled[:, n, 2:, :])
 
         regroup_chunk(0)
-        regroup_chunk(1)
         quantise_chunk(0)
+        regroup_chunk(1)
         copied = []
         ended = []
         for c in range(ALL_CHUNKS):
             n, part = divmod(c, CHUNKS)
             rows = slice(ROWS * part, ROWS * (part + 1))
-            if c + 2 < ALL_CHUNKS:
-                regroup_chunk(c + 2)
             for place, m in enumerate(tile_order):
                 if place == QUANTISE_AT and c + 1 < ALL_CHUNKS:
                     quantise_chunk(c + 1)
+                    if c + 2 < ALL_CHUNKS:
+                        regroup_chunk(c + 2)
                 if place == FINISH_AT and ended:
                     finish_map(ended.pop())
                 bank = banks.tile([P, CHUNK], F32, tag="bank")

@@ -29,9 +29,9 @@ OUT_ALL = OUT_Q + OUT_K + OUT_V
 TILES = OUT_ALL // P
 PSUM_BANKS = 8
 
-TENSOR_GROUP = 3
-SHARED_GROUP = 4
-VECTOR_GROUP = TILES - TENSOR_GROUP - SHARED_GROUP
+TENSOR_GROUP = 4
+GPSIMD_GROUP = 2
+VECTOR_GROUP = TILES - TENSOR_GROUP - GPSIMD_GROUP
 
 QUANTISE_AT = 6
 FINISH_AT = 3
@@ -44,15 +44,15 @@ def tile_pam_module_pa_kernel(
 ):
     nc = tc.nc
     tensor_tiles = list(range(TENSOR_GROUP))
-    shared_tiles = list(range(TENSOR_GROUP, TENSOR_GROUP + SHARED_GROUP))
-    vector_tiles = list(range(TENSOR_GROUP + SHARED_GROUP, TILES))
-    groups = [tensor_tiles, shared_tiles, vector_tiles]
+    gpsimd_tiles = list(range(TENSOR_GROUP, TENSOR_GROUP + GPSIMD_GROUP))
+    vector_tiles = list(range(TENSOR_GROUP + GPSIMD_GROUP, TILES))
+    groups = [tensor_tiles, gpsimd_tiles, vector_tiles]
     tile_order = [group[r] for r in range(TILES) for group in groups if r < len(group)]
 
     with ExitStack() as ctx:
         keep = ctx.enter_context(tc.tile_pool(name="keep", bufs=1))
         stage = ctx.enter_context(tc.tile_pool(name="stage", bufs=1))
-        products = ctx.enter_context(tc.tile_pool(name="products", bufs=4))
+        products = ctx.enter_context(tc.tile_pool(name="products", bufs=6))
         banks = ctx.enter_context(tc.psum_pool(name="banks", bufs=PSUM_BANKS - TENSOR_GROUP))
         column_banks = ctx.enter_context(tc.psum_pool(name="column_banks", bufs=TENSOR_GROUP))
         ctx.enter_context(tc.manual_schedule())
@@ -136,6 +136,7 @@ def tile_pam_module_pa_kernel(
         pooled = keep.tile([P, BATCH, TILES, HEIGHT + WIDTH], F32)
         bias = keep.tile([P, TILES], F32)
         column_bank = {}
+        map_sum = {}
 
         def multiply(bank, c, m, start, stop):
             for g in range(PASSES):
@@ -153,9 +154,11 @@ def tile_pam_module_pa_kernel(
             nc.vector.tensor_reduce(out=out, in_=eight_rows.rearrange("p i j -> p j i"), axis=AXIS_X, op=ADD)
 
         def finish_map(n):
+            for m in gpsimd_tiles:
+                sum_over_rows(col_sum[:, n, m, :], map_sum[n, m][:])
             nc.vector.tensor_reduce(
-                out=col_sum[:, n, TENSOR_GROUP:, :],
-                in_=col_part[:, n, TENSOR_GROUP:, :, :].rearrange("p m c j -> p m j c"),
+                out=col_sum[:, n, vector_tiles[0] :, :],
+                in_=col_part[:, n, vector_tiles[0] :, :, :].rearrange("p m c j -> p m j c"),
                 axis=AXIS_X,
                 op=ADD,
             )
@@ -182,7 +185,6 @@ def tile_pam_module_pa_kernel(
         regroup_chunk(0)
         quantise_chunk(0)
         regroup_chunk(1)
-        copied = []
         ended = []
         for c in range(ALL_CHUNKS):
             n, part = divmod(c, CHUNKS)
@@ -201,7 +203,11 @@ def tile_pam_module_pa_kernel(
                     nc.vector.tensor_reduce(out=row_sum[:, n, m, rows], in_=by_row, axis=AXIS_X, op=ADD)
                     sum_over_rows(col_part[:, n, m, part, :], by_row)
                     continue
-                product = products.tile([P, ROWS, WIDTH], F32, tag="product")
+                if m in gpsimd_tiles and part == 0:
+                    product = keep.tile([P, ROWS, WIDTH], F32, name="map_sum%d_%d" % (n, m))
+                    map_sum[n, m] = product
+                else:
+                    product = products.tile([P, ROWS, WIDTH], F32, tag="product")
                 for i in range(ROWS):
                     nc.scalar.activation(
                         out=product[:, i, :],
@@ -209,10 +215,9 @@ def tile_pam_module_pa_kernel(
                         func=COPY,
                         accum_out=row_sum[:, n, m, ROWS * part + i : ROWS * part + i + 1],
                     )
-                if m in shared_tiles:
-                    copied.append((col_part[:, n, m, part, :], product[:]))
-                    if len(copied) > 1:
-                        sum_over_rows(*copied.pop(0))
+                if m in gpsimd_tiles:
+                    if part > 0:
+                        nc.gpsimd.tensor_tensor(out=map_sum[n, m][:], in0=map_sum[n, m][:], in1=product[:], op=ADD)
                 else:
                     if part == 0:
                         column_bank[m] = column_banks.tile([P, CHUNK], F32, tag="column_bank", name="column_bank%d_%d" % (n, m))
@@ -225,5 +230,4 @@ def tile_pam_module_pa_kernel(
                 nc.vector.tensor_copy(out=bias[:], in_=bias_bank[:, 0:TILES])
             if part == CHUNKS - 1:
                 ended.append(n)
-        sum_over_rows(*copied.pop(0))
         finish_map(ended.pop())

@@ -28,6 +28,7 @@ OUT_Q, OUT_K, OUT_V = 128, 128, 1024
 OUT_ALL = OUT_Q + OUT_K + OUT_V
 TILES = OUT_ALL // P
 PSUM_BANKS = 8
+FOLD = 256
 
 TENSOR_GROUP = 4
 GPSIMD_GROUP = 2
@@ -73,17 +74,17 @@ def tile_pam_module_pa_kernel(
         nc.vector.memset(w_scales[:].bitcast(I32), 0)
         weights = ((Wq_words, Wq_scales, 0, OUT_Q), (Wk_words, Wk_scales, OUT_Q, OUT_K), (Wv_words, Wv_scales, OUT_Q + OUT_K, OUT_V))
         for words, scales, first, width in weights:
-            nc.sync.dma_start(
-                out=w_codes[:, :, first : first + width].bitcast(I32),
-                in_=words.rearrange("g p n t -> p g (n t)").bitcast(I32),
-            )
-        for words, scales, first, width in weights:
             scale_rows = scales.rearrange("g q n -> q g n")
             for quadrant in range(4):
                 nc.sync.dma_start(
                     out=w_scales[32 * quadrant : 32 * quadrant + 4, :, first : first + width].bitcast(I32),
                     in_=scale_rows[4 * quadrant : 4 * quadrant + 4].bitcast(I32),
                 )
+        for words, scales, first, width in weights:
+            nc.sync.dma_start(
+                out=w_codes[:, :, first : first + width].bitcast(I32),
+                in_=words.rearrange("g p n t -> p g (n t)").bitcast(I32),
+            )
 
         load_chunk(1)
         load_chunk(2)
@@ -138,24 +139,22 @@ def tile_pam_module_pa_kernel(
         column_bank = {}
         map_sum = {}
 
-        def multiply(bank, c, m, start, stop):
+        def multiply(bank, c, pixels, m, start, stop):
             for g in range(PASSES):
                 nc.tensor.matmul_mx(
                     out=bank[:],
                     lhsT=w_codes[:, g, P * m : P * (m + 1)].bitcast(FP8X4),
                     lhsT_scale=w_scales[:, g, P * m : P * (m + 1)],
-                    rhs=x_codes[c][:, g, :].bitcast(FP8X4),
-                    rhs_scale=x_scales[c][:, g, :],
+                    rhs=x_codes[c][:, g, pixels].bitcast(FP8X4),
+                    rhs_scale=x_scales[c][:, g, pixels],
                     start=start and g == 0,
                     stop=stop and g == PASSES - 1,
                 )
 
-        def sum_over_rows(out, eight_rows):
-            nc.vector.tensor_reduce(out=out, in_=eight_rows.rearrange("p i j -> p j i"), axis=AXIS_X, op=ADD)
+        def sum_over_rows(out, some_rows):
+            nc.vector.tensor_reduce(out=out, in_=some_rows.rearrange("p i j -> p j i"), axis=AXIS_X, op=ADD)
 
         def finish_map(n):
-            for m in gpsimd_tiles:
-                sum_over_rows(col_sum[:, n, m, :], map_sum[n, m][:])
             nc.vector.tensor_reduce(
                 out=col_sum[:, n, vector_tiles[0] :, :],
                 in_=col_part[:, n, vector_tiles[0] :, :, :].rearrange("p m c j -> p m j c"),
@@ -197,7 +196,7 @@ def tile_pam_module_pa_kernel(
                 if place == FINISH_AT and ended:
                     finish_map(ended.pop())
                 bank = banks.tile([P, CHUNK], F32, tag="bank")
-                multiply(bank, c, m, True, True)
+                multiply(bank, c, slice(0, CHUNK), m, True, True)
                 by_row = bank[:].rearrange("p (i j) -> p i j", j=WIDTH)
                 if m in vector_tiles:
                     nc.vector.tensor_reduce(out=row_sum[:, n, m, rows], in_=by_row, axis=AXIS_X, op=ADD)
@@ -216,12 +215,18 @@ def tile_pam_module_pa_kernel(
                         accum_out=row_sum[:, n, m, ROWS * part + i : ROWS * part + i + 1],
                     )
                 if m in gpsimd_tiles:
+                    total = map_sum[n, m]
                     if part > 0:
-                        nc.gpsimd.tensor_tensor(out=map_sum[n, m][:], in0=map_sum[n, m][:], in1=product[:], op=ADD)
+                        nc.gpsimd.tensor_tensor(out=total[:], in0=total[:], in1=product[:], op=ADD)
+                    if part == CHUNKS - 1:
+                        nc.gpsimd.tensor_tensor(out=total[:, 0:4, :], in0=total[:, 0:4, :], in1=total[:, 4:8, :], op=ADD)
+                        nc.gpsimd.tensor_tensor(out=total[:, 0:2, :], in0=total[:, 0:2, :], in1=total[:, 2:4, :], op=ADD)
+                        nc.gpsimd.tensor_tensor(out=col_sum[:, n, m, :], in0=total[:, 0, :], in1=total[:, 1, :], op=ADD)
                 else:
                     if part == 0:
-                        column_bank[m] = column_banks.tile([P, CHUNK], F32, tag="column_bank", name="column_bank%d_%d" % (n, m))
-                    multiply(column_bank[m], c, m, part == 0, part == CHUNKS - 1)
+                        column_bank[m] = column_banks.tile([P, FOLD], F32, tag="column_bank", name="column_bank%d_%d" % (n, m))
+                    multiply(column_bank[m], c, slice(0, FOLD), m, part == 0, False)
+                    multiply(column_bank[m], c, slice(FOLD, CHUNK), m, False, part == CHUNKS - 1)
                     if part == CHUNKS - 1:
                         sum_over_rows(col_sum[:, n, m, :], column_bank[m][:].rearrange("p (i j) -> p i j", j=WIDTH))
             if c == 0:

@@ -28,7 +28,6 @@ OUT_Q, OUT_K, OUT_V = 128, 128, 1024
 OUT_ALL = OUT_Q + OUT_K + OUT_V
 TILES = OUT_ALL // P
 PSUM_BANKS = 8
-FOLD = 256
 
 TENSOR_GROUP = 4
 GPSIMD_GROUP = 2
@@ -72,19 +71,18 @@ def tile_pam_module_pa_kernel(
         w_codes = keep.tile([P, PASSES, OUT_ALL], U32, align_bytes=64)
         w_scales = keep.tile([P, PASSES, OUT_ALL], U8, align_bytes=64)
         nc.vector.memset(w_scales[:].bitcast(I32), 0)
-        weights = ((Wq_words, Wq_scales, 0, OUT_Q), (Wk_words, Wk_scales, OUT_Q, OUT_K), (Wv_words, Wv_scales, OUT_Q + OUT_K, OUT_V))
+        weights = ((Wq_words, Wq_scales, 0, OUT_Q), (Wv_words, Wv_scales, OUT_Q + OUT_K, OUT_V), (Wk_words, Wk_scales, OUT_Q, OUT_K))
         for words, scales, first, width in weights:
+            nc.sync.dma_start(
+                out=w_codes[:, :, first : first + width].bitcast(I32),
+                in_=words.rearrange("g p n t -> p g (n t)").bitcast(I32),
+            )
             scale_rows = scales.rearrange("g q n -> q g n")
             for quadrant in range(4):
                 nc.sync.dma_start(
                     out=w_scales[32 * quadrant : 32 * quadrant + 4, :, first : first + width].bitcast(I32),
                     in_=scale_rows[4 * quadrant : 4 * quadrant + 4].bitcast(I32),
                 )
-        for words, scales, first, width in weights:
-            nc.sync.dma_start(
-                out=w_codes[:, :, first : first + width].bitcast(I32),
-                in_=words.rearrange("g p n t -> p g (n t)").bitcast(I32),
-            )
 
         load_chunk(1)
         load_chunk(2)
@@ -139,22 +137,24 @@ def tile_pam_module_pa_kernel(
         column_bank = {}
         map_sum = {}
 
-        def multiply(bank, c, pixels, m, start, stop):
+        def multiply(bank, c, m, start, stop):
             for g in range(PASSES):
                 nc.tensor.matmul_mx(
                     out=bank[:],
                     lhsT=w_codes[:, g, P * m : P * (m + 1)].bitcast(FP8X4),
                     lhsT_scale=w_scales[:, g, P * m : P * (m + 1)],
-                    rhs=x_codes[c][:, g, pixels].bitcast(FP8X4),
-                    rhs_scale=x_scales[c][:, g, pixels],
+                    rhs=x_codes[c][:, g, :].bitcast(FP8X4),
+                    rhs_scale=x_scales[c][:, g, :],
                     start=start and g == 0,
                     stop=stop and g == PASSES - 1,
                 )
 
-        def sum_over_rows(out, some_rows):
-            nc.vector.tensor_reduce(out=out, in_=some_rows.rearrange("p i j -> p j i"), axis=AXIS_X, op=ADD)
+        def sum_over_rows(out, eight_rows):
+            nc.vector.tensor_reduce(out=out, in_=eight_rows.rearrange("p i j -> p j i"), axis=AXIS_X, op=ADD)
 
         def finish_map(n):
+            for m in gpsimd_tiles:
+                sum_over_rows(col_sum[:, n, m, :], map_sum[n, m][:])
             nc.vector.tensor_reduce(
                 out=col_sum[:, n, vector_tiles[0] :, :],
                 in_=col_part[:, n, vector_tiles[0] :, :, :].rearrange("p m c j -> p m j c"),
@@ -196,7 +196,7 @@ def tile_pam_module_pa_kernel(
                 if place == FINISH_AT and ended:
                     finish_map(ended.pop())
                 bank = banks.tile([P, CHUNK], F32, tag="bank")
-                multiply(bank, c, slice(0, CHUNK), m, True, True)
+                multiply(bank, c, m, True, True)
                 by_row = bank[:].rearrange("p (i j) -> p i j", j=WIDTH)
                 if m in vector_tiles:
                     nc.vector.tensor_reduce(out=row_sum[:, n, m, rows], in_=by_row, axis=AXIS_X, op=ADD)
@@ -215,18 +215,12 @@ def tile_pam_module_pa_kernel(
                         accum_out=row_sum[:, n, m, ROWS * part + i : ROWS * part + i + 1],
                     )
                 if m in gpsimd_tiles:
-                    total = map_sum[n, m]
                     if part > 0:
-                        nc.gpsimd.tensor_tensor(out=total[:], in0=total[:], in1=product[:], op=ADD)
-                    if part == CHUNKS - 1:
-                        nc.gpsimd.tensor_tensor(out=total[:, 0:4, :], in0=total[:, 0:4, :], in1=total[:, 4:8, :], op=ADD)
-                        nc.gpsimd.tensor_tensor(out=total[:, 0:2, :], in0=total[:, 0:2, :], in1=total[:, 2:4, :], op=ADD)
-                        nc.gpsimd.tensor_tensor(out=col_sum[:, n, m, :], in0=total[:, 0, :], in1=total[:, 1, :], op=ADD)
+                        nc.gpsimd.tensor_tensor(out=map_sum[n, m][:], in0=map_sum[n, m][:], in1=product[:], op=ADD)
                 else:
                     if part == 0:
-                        column_bank[m] = column_banks.tile([P, FOLD], F32, tag="column_bank", name="column_bank%d_%d" % (n, m))
-                    multiply(column_bank[m], c, slice(0, FOLD), m, part == 0, False)
-                    multiply(column_bank[m], c, slice(FOLD, CHUNK), m, False, part == CHUNKS - 1)
+                        column_bank[m] = column_banks.tile([P, CHUNK], F32, tag="column_bank", name="column_bank%d_%d" % (n, m))
+                    multiply(column_bank[m], c, m, part == 0, part == CHUNKS - 1)
                     if part == CHUNKS - 1:
                         sum_over_rows(col_sum[:, n, m, :], column_bank[m][:].rearrange("p (i j) -> p i j", j=WIDTH))
             if c == 0:

@@ -30,11 +30,9 @@ TILES = OUT_ALL // P
 PSUM_BANKS = 8
 
 TENSOR_GROUP = 4
-GPSIMD_GROUP = 2
-VECTOR_GROUP = TILES - TENSOR_GROUP - GPSIMD_GROUP
-
-QUANTISE_AT = 6
-FINISH_AT = 3
+GPSIMD_GROUP = 3
+SHARED_GROUP = 1
+VECTOR_GROUP = TILES - TENSOR_GROUP - GPSIMD_GROUP - SHARED_GROUP
 
 FLOPS = 2 * OUT_ALL * CHANNELS * BATCH * PIXELS
 
@@ -45,9 +43,9 @@ def tile_pam_module_pa_kernel(
     nc = tc.nc
     tensor_tiles = list(range(TENSOR_GROUP))
     gpsimd_tiles = list(range(TENSOR_GROUP, TENSOR_GROUP + GPSIMD_GROUP))
-    vector_tiles = list(range(TENSOR_GROUP + GPSIMD_GROUP, TILES))
-    groups = [tensor_tiles, gpsimd_tiles, vector_tiles]
-    tile_order = [group[r] for r in range(TILES) for group in groups if r < len(group)]
+    shared_tiles = list(range(TENSOR_GROUP + GPSIMD_GROUP, TILES - VECTOR_GROUP))
+    vector_tiles = list(range(TILES - VECTOR_GROUP, TILES))
+    tile_order = gpsimd_tiles + shared_tiles + vector_tiles + tensor_tiles
 
     with ExitStack() as ctx:
         keep = ctx.enter_context(tc.tile_pool(name="keep", bufs=1))
@@ -60,23 +58,22 @@ def tile_pam_module_pa_kernel(
         x_view = x.rearrange("n (g p t) h w -> n g p t (h w)", g=PASSES, p=P, t=PACK)
         raw = {}
 
-        def load_chunk(c):
+        def load_half_chunk(c, g):
             n, part = divmod(c, CHUNKS)
+            raw[c, g] = keep.tile([P, PACK, CHUNK], BF16, name="raw%d_%d" % (c, g))
+            nc.sync.dma_start(out=raw[c, g][:], in_=x_view[n, g, :, :, CHUNK * part : CHUNK * (part + 1)])
+
+        def load_chunk(c):
             for g in range(PASSES):
-                raw[c, g] = keep.tile([P, PACK, CHUNK], BF16, name="raw%d_%d" % (c, g))
-                nc.sync.dma_start(out=raw[c, g][:], in_=x_view[n, g, :, :, CHUNK * part : CHUNK * (part + 1)])
+                load_half_chunk(c, g)
 
         load_chunk(0)
 
         w_codes = keep.tile([P, PASSES, OUT_ALL], U32, align_bytes=64)
         w_scales = keep.tile([P, PASSES, OUT_ALL], U8, align_bytes=64)
         nc.vector.memset(w_scales[:].bitcast(I32), 0)
-        weights = ((Wq_words, Wq_scales, 0, OUT_Q), (Wv_words, Wv_scales, OUT_Q + OUT_K, OUT_V), (Wk_words, Wk_scales, OUT_Q, OUT_K))
-        for words, scales, first, width in weights:
-            nc.sync.dma_start(
-                out=w_codes[:, :, first : first + width].bitcast(I32),
-                in_=words.rearrange("g p n t -> p g (n t)").bitcast(I32),
-            )
+
+        def load_scales(scales, first, width):
             scale_rows = scales.rearrange("g q n -> q g n")
             for quadrant in range(4):
                 nc.sync.dma_start(
@@ -84,7 +81,25 @@ def tile_pam_module_pa_kernel(
                     in_=scale_rows[4 * quadrant : 4 * quadrant + 4].bitcast(I32),
                 )
 
-        load_chunk(1)
+        def load_words(words, first, start, stop):
+            nc.sync.dma_start(
+                out=w_codes[:, :, first + start : first + stop].bitcast(I32),
+                in_=words[:, :, start:stop, :].rearrange("g p n t -> p g (n t)").bitcast(I32),
+            )
+
+        first_v = OUT_Q + OUT_K
+        v_of_tensor_group = P * TENSOR_GROUP - first_v
+        v_of_gpsimd_group = v_of_tensor_group + P * GPSIMD_GROUP
+        load_scales(Wv_scales, first_v, OUT_V)
+        load_words(Wv_words, first_v, v_of_tensor_group, v_of_gpsimd_group)
+        load_half_chunk(1, 0)
+        load_words(Wv_words, first_v, v_of_gpsimd_group, OUT_V)
+        load_half_chunk(1, 1)
+        load_words(Wq_words, 0, 0, OUT_Q)
+        load_scales(Wq_scales, 0, OUT_Q)
+        load_words(Wk_words, OUT_Q, 0, OUT_K)
+        load_scales(Wk_scales, OUT_Q, OUT_K)
+        load_words(Wv_words, first_v, 0, v_of_tensor_group)
         load_chunk(2)
 
         bias_rows = keep.tile([P, P], BF16)
@@ -105,20 +120,10 @@ def tile_pam_module_pa_kernel(
         def regroup_chunk(c):
             grouped[c] = stage.tile([P, PASSES, CHUNK, PACK], BF16, tag="grouped", name="grouped%d" % c, align_bytes=64)
             for g in range(PASSES):
-                if c == 0:
-                    nc.vector.tensor_copy(
-                        out=grouped[c][:, g].rearrange("p (w i) t -> p w t i", i=4),
-                        in_=raw[c, g][:].rearrange("p t (w i) -> p w t i", i=4),
-                    )
-                else:
-                    nc.gpsimd.tensor_scalar(
-                        out=grouped[c][:, g],
-                        in0=raw[c, g][:].rearrange("p t w -> p w t"),
-                        scalar1=1.0,
-                        scalar2=0.0,
-                        op0=MULT,
-                        op1=ADD,
-                    )
+                nc.vector.tensor_copy(
+                    out=grouped[c][:, g].rearrange("p (w i) t -> p w t i", i=4),
+                    in_=raw[c, g][:].rearrange("p t (w i) -> p w t i", i=4),
+                )
 
         def quantise_chunk(c):
             x_codes[c] = keep.tile([P, PASSES, CHUNK], U32, name="x_codes%d" % c, align_bytes=64)
@@ -156,8 +161,8 @@ def tile_pam_module_pa_kernel(
             for m in gpsimd_tiles:
                 sum_over_rows(col_sum[:, n, m, :], map_sum[n, m][:])
             nc.vector.tensor_reduce(
-                out=col_sum[:, n, vector_tiles[0] :, :],
-                in_=col_part[:, n, vector_tiles[0] :, :, :].rearrange("p m c j -> p m j c"),
+                out=col_sum[:, n, shared_tiles[0] :, :],
+                in_=col_part[:, n, shared_tiles[0] :, :, :].rearrange("p m c j -> p m j c"),
                 axis=AXIS_X,
                 op=ADD,
             )
@@ -188,13 +193,14 @@ def tile_pam_module_pa_kernel(
         for c in range(ALL_CHUNKS):
             n, part = divmod(c, CHUNKS)
             rows = slice(ROWS * part, ROWS * (part + 1))
-            for place, m in enumerate(tile_order):
-                if place == QUANTISE_AT and c + 1 < ALL_CHUNKS:
-                    quantise_chunk(c + 1)
+            for m in tile_order:
+                if m == tensor_tiles[0]:
+                    if c + 1 < ALL_CHUNKS:
+                        quantise_chunk(c + 1)
                     if c + 2 < ALL_CHUNKS:
                         regroup_chunk(c + 2)
-                if place == FINISH_AT and ended:
-                    finish_map(ended.pop())
+                    if ended:
+                        finish_map(ended.pop())
                 bank = banks.tile([P, CHUNK], F32, tag="bank")
                 multiply(bank, c, m, True, True)
                 by_row = bank[:].rearrange("p (i j) -> p i j", j=WIDTH)
@@ -202,6 +208,8 @@ def tile_pam_module_pa_kernel(
                     nc.vector.tensor_reduce(out=row_sum[:, n, m, rows], in_=by_row, axis=AXIS_X, op=ADD)
                     sum_over_rows(col_part[:, n, m, part, :], by_row)
                     continue
+                if m in shared_tiles:
+                    sum_over_rows(col_part[:, n, m, part, :], by_row)
                 if m in gpsimd_tiles and part == 0:
                     product = keep.tile([P, ROWS, WIDTH], F32, name="map_sum%d_%d" % (n, m))
                     map_sum[n, m] = product
@@ -217,7 +225,7 @@ def tile_pam_module_pa_kernel(
                 if m in gpsimd_tiles:
                     if part > 0:
                         nc.gpsimd.tensor_tensor(out=map_sum[n, m][:], in0=map_sum[n, m][:], in1=product[:], op=ADD)
-                else:
+                elif m in tensor_tiles:
                     if part == 0:
                         column_bank[m] = column_banks.tile([P, CHUNK], F32, tag="column_bank", name="column_bank%d_%d" % (n, m))
                     multiply(column_bank[m], c, m, part == 0, part == CHUNKS - 1)

@@ -30,9 +30,14 @@ TILES = OUT_ALL // P
 PSUM_BANKS = 8
 
 TENSOR_GROUP = 4
-GPSIMD_GROUP = 3
+GPSIMD_GROUP = 2
 SHARED_GROUP = 1
 VECTOR_GROUP = TILES - TENSOR_GROUP - GPSIMD_GROUP - SHARED_GROUP
+SCALAR_ROWS = 6
+FOLD = 256
+
+VECTOR_PIXELS = 256
+OVERLAP = 4
 
 FLOPS = 2 * OUT_ALL * CHANNELS * BATCH * PIXELS
 
@@ -45,7 +50,10 @@ def tile_pam_module_pa_kernel(
     gpsimd_tiles = list(range(TENSOR_GROUP, TENSOR_GROUP + GPSIMD_GROUP))
     shared_tiles = list(range(TENSOR_GROUP + GPSIMD_GROUP, TILES - VECTOR_GROUP))
     vector_tiles = list(range(TILES - VECTOR_GROUP, TILES))
-    tile_order = gpsimd_tiles + shared_tiles + vector_tiles + tensor_tiles
+    first_column_tile = shared_tiles[0]
+    scalar_first_half = gpsimd_tiles + shared_tiles
+    first_half = [group[r] for r in range(TILES) for group in (vector_tiles, scalar_first_half) if r < len(group)]
+    tile_order = first_half + tensor_tiles
 
     with ExitStack() as ctx:
         keep = ctx.enter_context(tc.tile_pool(name="keep", bufs=1))
@@ -58,20 +66,17 @@ def tile_pam_module_pa_kernel(
         x_view = x.rearrange("n (g p t) h w -> n g p t (h w)", g=PASSES, p=P, t=PACK)
         raw = {}
 
-        def load_half_chunk(c, g):
-            n, part = divmod(c, CHUNKS)
-            raw[c, g] = keep.tile([P, PACK, CHUNK], BF16, name="raw%d_%d" % (c, g))
-            nc.sync.dma_start(out=raw[c, g][:], in_=x_view[n, g, :, :, CHUNK * part : CHUNK * (part + 1)])
-
         def load_chunk(c):
+            n, part = divmod(c, CHUNKS)
+            raw[c] = keep.tile([P, PASSES, PACK, CHUNK], BF16, name="raw%d" % c)
             for g in range(PASSES):
-                load_half_chunk(c, g)
+                nc.sync.dma_start(out=raw[c][:, g], in_=x_view[n, g, :, :, CHUNK * part : CHUNK * (part + 1)])
 
         load_chunk(0)
 
         w_codes = keep.tile([P, PASSES, OUT_ALL], U32, align_bytes=64)
         w_scales = keep.tile([P, PASSES, OUT_ALL], U8, align_bytes=64)
-        nc.vector.memset(w_scales[:].bitcast(I32), 0)
+        nc.gpsimd.memset(w_scales[:].bitcast(F32), 0.0)
 
         def load_scales(scales, first, width):
             scale_rows = scales.rearrange("g q n -> q g n")
@@ -89,12 +94,9 @@ def tile_pam_module_pa_kernel(
 
         first_v = OUT_Q + OUT_K
         v_of_tensor_group = P * TENSOR_GROUP - first_v
-        v_of_gpsimd_group = v_of_tensor_group + P * GPSIMD_GROUP
         load_scales(Wv_scales, first_v, OUT_V)
-        load_words(Wv_words, first_v, v_of_tensor_group, v_of_gpsimd_group)
-        load_half_chunk(1, 0)
-        load_words(Wv_words, first_v, v_of_gpsimd_group, OUT_V)
-        load_half_chunk(1, 1)
+        load_words(Wv_words, first_v, v_of_tensor_group, OUT_V)
+        load_chunk(1)
         load_words(Wq_words, 0, 0, OUT_Q)
         load_scales(Wq_scales, 0, OUT_Q)
         load_words(Wk_words, OUT_Q, 0, OUT_K)
@@ -117,13 +119,28 @@ def tile_pam_module_pa_kernel(
         x_codes = {}
         x_scales = {}
 
+        def regroup_by_vector(c, passes, stop):
+            nc.vector.tensor_copy(
+                out=grouped[c][:, passes, 0:stop, :].rearrange("p g (w i) t -> p g w t i", i=4),
+                in_=raw[c][:, passes, :, 0:stop].rearrange("p g t (w i) -> p g w t i", i=4),
+            )
+
         def regroup_chunk(c):
             grouped[c] = stage.tile([P, PASSES, CHUNK, PACK], BF16, tag="grouped", name="grouped%d" % c, align_bytes=64)
-            for g in range(PASSES):
-                nc.vector.tensor_copy(
-                    out=grouped[c][:, g].rearrange("p (w i) t -> p w t i", i=4),
-                    in_=raw[c, g][:].rearrange("p t (w i) -> p w t i", i=4),
-                )
+            if c == 0:
+                for g in range(PASSES):
+                    regroup_by_vector(c, slice(g, g + 1), CHUNK)
+                return
+            regroup_by_vector(c, slice(0, PASSES), VECTOR_PIXELS)
+            start = VECTOR_PIXELS - OVERLAP
+            nc.gpsimd.tensor_scalar(
+                out=grouped[c][:, :, start:, :],
+                in0=raw[c][:, :, :, start:].rearrange("p g t w -> p g w t"),
+                scalar1=1.0,
+                scalar2=0.0,
+                op0=MULT,
+                op1=ADD,
+            )
 
         def quantise_chunk(c):
             x_codes[c] = keep.tile([P, PASSES, CHUNK], U32, name="x_codes%d" % c, align_bytes=64)
@@ -142,99 +159,128 @@ def tile_pam_module_pa_kernel(
         column_bank = {}
         map_sum = {}
 
-        def multiply(bank, c, m, start, stop):
+        def multiply(out, c, m, first, width, start, stop):
             for g in range(PASSES):
                 nc.tensor.matmul_mx(
-                    out=bank[:],
+                    out=out,
                     lhsT=w_codes[:, g, P * m : P * (m + 1)].bitcast(FP8X4),
                     lhsT_scale=w_scales[:, g, P * m : P * (m + 1)],
-                    rhs=x_codes[c][:, g, :].bitcast(FP8X4),
-                    rhs_scale=x_scales[c][:, g, :],
+                    rhs=x_codes[c][:, g, first : first + width].bitcast(FP8X4),
+                    rhs_scale=x_scales[c][:, g, first : first + width],
                     start=start and g == 0,
                     stop=stop and g == PASSES - 1,
                 )
 
-        def sum_over_rows(out, eight_rows):
-            nc.vector.tensor_reduce(out=out, in_=eight_rows.rearrange("p i j -> p j i"), axis=AXIS_X, op=ADD)
+        def sum_over_rows(out, some_rows):
+            nc.vector.tensor_reduce(out=out, in_=some_rows.rearrange("p i j -> p j i"), axis=AXIS_X, op=ADD)
 
-        def finish_map(n):
-            for m in gpsimd_tiles:
-                sum_over_rows(col_sum[:, n, m, :], map_sum[n, m][:])
-            nc.vector.tensor_reduce(
-                out=col_sum[:, n, shared_tiles[0] :, :],
-                in_=col_part[:, n, shared_tiles[0] :, :, :].rearrange("p m c j -> p m j c"),
-                axis=AXIS_X,
-                op=ADD,
-            )
+        def sum_along_rows(out, some_rows):
+            nc.vector.tensor_reduce(out=out, in_=some_rows, axis=AXIS_X, op=ADD)
+
+        def store_means(n, lo, hi):
             nc.vector.scalar_tensor_tensor(
-                out=pooled[:, n, :, 0:HEIGHT],
-                in0=row_sum[:, n, :, :],
+                out=pooled[:, n, lo:hi, 0:HEIGHT],
+                in0=row_sum[:, n, lo:hi, :],
                 scalar=1.0 / WIDTH,
-                in1=bias[:].unsqueeze(2).to_broadcast([P, TILES, HEIGHT]),
+                in1=bias[:, lo:hi].unsqueeze(2).to_broadcast([P, hi - lo, HEIGHT]),
                 op0=MULT,
                 op1=ADD,
             )
             nc.vector.scalar_tensor_tensor(
-                out=pooled[:, n, :, HEIGHT:],
-                in0=col_sum[:, n, :, :],
+                out=pooled[:, n, lo:hi, HEIGHT:],
+                in0=col_sum[:, n, lo:hi, :],
                 scalar=1.0 / HEIGHT,
-                in1=bias[:].unsqueeze(2).to_broadcast([P, TILES, WIDTH]),
+                in1=bias[:, lo:hi].unsqueeze(2).to_broadcast([P, hi - lo, WIDTH]),
                 op0=MULT,
                 op1=ADD,
             )
-            nc.sync.dma_start(out=out_0[n], in_=pooled[:, n, 0, :])
-            nc.sync.dma_start(out=out_1[n], in_=pooled[:, n, 1, :])
-            nc.sync.dma_start(out=out_2[n].rearrange("(m p) f -> p m f", p=P), in_=pooled[:, n, 2:, :])
+            if lo == 0:
+                nc.sync.dma_start(out=out_0[n], in_=pooled[:, n, 0, :])
+                nc.sync.dma_start(out=out_1[n], in_=pooled[:, n, 1, :])
+            first = max(lo, 2)
+            nc.sync.dma_start(
+                out=out_2[n].rearrange("(m p) f -> p m f", p=P)[:, first - 2 : hi - 2, :], in_=pooled[:, n, first:hi, :]
+            )
+
+        def closing_steps(n):
+            steps = [lambda m=m: sum_over_rows(col_sum[:, n, m, :], map_sum[n, m][:]) for m in gpsimd_tiles]
+            steps.append(
+                lambda: nc.vector.tensor_reduce(
+                    out=col_sum[:, n, first_column_tile:, :],
+                    in_=col_part[:, n, first_column_tile:, :, :].rearrange("p m c j -> p m j c"),
+                    axis=AXIS_X,
+                    op=ADD,
+                )
+            )
+            steps.append(lambda: store_means(n, TENSOR_GROUP, TILES))
+            return steps
 
         regroup_chunk(0)
         quantise_chunk(0)
         regroup_chunk(1)
-        ended = []
+        waiting = []
         for c in range(ALL_CHUNKS):
             n, part = divmod(c, CHUNKS)
             rows = slice(ROWS * part, ROWS * (part + 1))
+            last_of_map = part == CHUNKS - 1
+            last_of_all = c == ALL_CHUNKS - 1
+            after_scalar = []
             for m in tile_order:
                 if m == tensor_tiles[0]:
-                    if c + 1 < ALL_CHUNKS:
+                    if waiting:
+                        waiting.pop(0)()
+                    for read in after_scalar:
+                        read()
+                    if not last_of_all:
                         quantise_chunk(c + 1)
                     if c + 2 < ALL_CHUNKS:
                         regroup_chunk(c + 2)
-                    if ended:
-                        finish_map(ended.pop())
+                    if last_of_all:
+                        for step in waiting + closing_steps(n):
+                            step()
                 bank = banks.tile([P, CHUNK], F32, tag="bank")
-                multiply(bank, c, m, True, True)
+                multiply(bank[:], c, m, 0, CHUNK, True, True)
                 by_row = bank[:].rearrange("p (i j) -> p i j", j=WIDTH)
                 if m in vector_tiles:
-                    nc.vector.tensor_reduce(out=row_sum[:, n, m, rows], in_=by_row, axis=AXIS_X, op=ADD)
+                    sum_along_rows(row_sum[:, n, m, rows], by_row)
                     sum_over_rows(col_part[:, n, m, part, :], by_row)
                     continue
-                if m in shared_tiles:
-                    sum_over_rows(col_part[:, n, m, part, :], by_row)
                 if m in gpsimd_tiles and part == 0:
                     product = keep.tile([P, ROWS, WIDTH], F32, name="map_sum%d_%d" % (n, m))
                     map_sum[n, m] = product
                 else:
                     product = products.tile([P, ROWS, WIDTH], F32, tag="product")
-                for i in range(ROWS):
+                scalar_rows = SCALAR_ROWS if m in shared_tiles else ROWS
+                for i in range(scalar_rows):
                     nc.scalar.activation(
                         out=product[:, i, :],
                         in_=by_row[:, i, :],
                         func=COPY,
                         accum_out=row_sum[:, n, m, ROWS * part + i : ROWS * part + i + 1],
                     )
-                if m in gpsimd_tiles:
+                if m in shared_tiles:
+                    after_scalar.append(
+                        lambda m=m, by_row=by_row: sum_along_rows(
+                            row_sum[:, n, m, ROWS * part + SCALAR_ROWS : ROWS * (part + 1)], by_row[:, SCALAR_ROWS:, :]
+                        )
+                    )
+                    after_scalar.append(lambda m=m, by_row=by_row: sum_over_rows(col_part[:, n, m, part, :], by_row))
+                elif m in gpsimd_tiles:
                     if part > 0:
                         nc.gpsimd.tensor_tensor(out=map_sum[n, m][:], in0=map_sum[n, m][:], in1=product[:], op=ADD)
-                elif m in tensor_tiles:
+                else:
                     if part == 0:
-                        column_bank[m] = column_banks.tile([P, CHUNK], F32, tag="column_bank", name="column_bank%d_%d" % (n, m))
-                    multiply(column_bank[m], c, m, part == 0, part == CHUNKS - 1)
-                    if part == CHUNKS - 1:
+                        column_bank[m] = column_banks.tile([P, FOLD], F32, tag="column_bank", name="column_bank%d_%d" % (n, m))
+                    for first in range(0, CHUNK, FOLD):
+                        multiply(column_bank[m][:], c, m, first, FOLD, part == 0 and first == 0, last_of_map and first == CHUNK - FOLD)
+                    if last_of_map:
                         sum_over_rows(col_sum[:, n, m, :], column_bank[m][:].rearrange("p (i j) -> p i j", j=WIDTH))
             if c == 0:
                 bias_bank = banks.tile([P, P], BF16, tag="bank")
                 nc.tensor.transpose(bias_bank[:], bias_rows[:], identity[:])
                 nc.vector.tensor_copy(out=bias[:], in_=bias_bank[:, 0:TILES])
-            if part == CHUNKS - 1:
-                ended.append(n)
-        finish_map(ended.pop())
+            if last_of_map:
+                if last_of_all:
+                    store_means(n, 0, TENSOR_GROUP)
+                else:
+                    waiting = closing_steps(n) + [lambda n=n: store_means(n, 0, TENSOR_GROUP)]

@@ -202,18 +202,23 @@ def tile_pam_module_pa_kernel(
                 out=out_2[n].rearrange("(m p) f -> p m f", p=P)[:, first - 2 : hi - 2, :], in_=pooled[:, n, first:hi, :]
             )
 
-        def closing_steps(n):
-            steps = [lambda m=m: sum_over_rows(col_sum[:, n, m, :], map_sum[n, m][:]) for m in gpsimd_tiles]
-            steps.append(
-                lambda: nc.vector.tensor_reduce(
-                    out=col_sum[:, n, first_column_tile:, :],
-                    in_=col_part[:, n, first_column_tile:, :, :].rearrange("p m c j -> p m j c"),
-                    axis=AXIS_X,
-                    op=ADD,
+        def fold_map_sum(n):
+            for half in (ROWS // 2, ROWS // 4):
+                nc.gpsimd.tensor_tensor(
+                    out=map_sum[n][:, :, 0:half, :], in0=map_sum[n][:, :, 0:half, :], in1=map_sum[n][:, :, half : 2 * half, :], op=ADD
                 )
+            nc.gpsimd.tensor_tensor(
+                out=col_sum[:, n, gpsimd_tiles[0] : first_column_tile, :], in0=map_sum[n][:, :, 0, :], in1=map_sum[n][:, :, 1, :], op=ADD
             )
-            steps.append(lambda: store_means(n, TENSOR_GROUP, TILES))
-            return steps
+
+        def add_chunks_up(n, lo, hi):
+            nc.vector.tensor_reduce(
+                out=col_sum[:, n, lo:hi, :], in_=col_part[:, n, lo:hi, :, :].rearrange("p m c j -> p m j c"), axis=AXIS_X, op=ADD
+            )
+
+        def closing_steps(n):
+            middle = (first_column_tile + TILES) // 2
+            return [lambda: add_chunks_up(n, first_column_tile, middle), lambda: add_chunks_up(n, middle, TILES)]
 
         regroup_chunk(0)
         quantise_chunk(0)
@@ -235,9 +240,14 @@ def tile_pam_module_pa_kernel(
                         quantise_chunk(c + 1)
                     if c + 2 < ALL_CHUNKS:
                         regroup_chunk(c + 2)
-                    if last_of_all:
-                        for step in waiting + closing_steps(n):
+                    else:
+                        for step in waiting:
                             step()
+                        waiting = []
+                    if last_of_all:
+                        for step in closing_steps(n):
+                            step()
+                        store_means(n, first_column_tile, TILES)
                 bank = banks.tile([P, CHUNK], F32, tag="bank")
                 multiply(bank[:], c, m, 0, CHUNK, True, True)
                 by_row = bank[:].rearrange("p (i j) -> p i j", j=WIDTH)
@@ -246,11 +256,16 @@ def tile_pam_module_pa_kernel(
                     sum_over_rows(col_part[:, n, m, part, :], by_row)
                     continue
                 if m in gpsimd_tiles and part == 0:
-                    product = keep.tile([P, ROWS, WIDTH], F32, name="map_sum%d_%d" % (n, m))
-                    map_sum[n, m] = product
+                    if m == gpsimd_tiles[0]:
+                        map_sum[n] = keep.tile([P, GPSIMD_GROUP, ROWS, WIDTH], F32, name="map_sum%d" % n)
+                    product = map_sum[n][:, m - gpsimd_tiles[0]]
                 else:
-                    product = products.tile([P, ROWS, WIDTH], F32, tag="product")
-                scalar_rows = SCALAR_ROWS if m in shared_tiles else ROWS
+                    product_tile = products.tile([P, ROWS, WIDTH], F32, tag="product")
+                    product = product_tile[:]
+                very_last = last_of_all and m == tile_order[-1]
+                scalar_rows = SCALAR_ROWS if m in shared_tiles else 0 if very_last else ROWS
+                if very_last:
+                    sum_along_rows(row_sum[:, n, m, rows], by_row)
                 for i in range(scalar_rows):
                     nc.scalar.activation(
                         out=product[:, i, :],
@@ -267,7 +282,13 @@ def tile_pam_module_pa_kernel(
                     after_scalar.append(lambda m=m, by_row=by_row: sum_over_rows(col_part[:, n, m, part, :], by_row))
                 elif m in gpsimd_tiles:
                     if part > 0:
-                        nc.gpsimd.tensor_tensor(out=map_sum[n, m][:], in0=map_sum[n, m][:], in1=product[:], op=ADD)
+                        so_far = map_sum[n][:, m - gpsimd_tiles[0]]
+                        nc.gpsimd.tensor_tensor(out=so_far, in0=so_far, in1=product, op=ADD)
+                    if m == gpsimd_tiles[-1]:
+                        if part == 0 and n > 0:
+                            fold_map_sum(n - 1)
+                        if last_of_all:
+                            fold_map_sum(n)
                 else:
                     if part == 0:
                         column_bank[m] = column_banks.tile([P, FOLD], F32, tag="column_bank", name="column_bank%d_%d" % (n, m))
@@ -281,6 +302,8 @@ def tile_pam_module_pa_kernel(
                 nc.vector.tensor_copy(out=bias[:], in_=bias_bank[:, 0:TILES])
             if last_of_map:
                 if last_of_all:
+                    store_means(n, TENSOR_GROUP, first_column_tile)
                     store_means(n, 0, TENSOR_GROUP)
                 else:
-                    waiting = closing_steps(n) + [lambda n=n: store_means(n, 0, TENSOR_GROUP)]
+                    waiting = [lambda n=n: store_means(n, 0, TENSOR_GROUP)] + closing_steps(n)
+                    waiting.append(lambda n=n: store_means(n, TENSOR_GROUP, TILES))

@@ -128,8 +128,10 @@ def tile_pam_module_pa_kernel(
         def regroup_chunk(c):
             grouped[c] = stage.tile([P, PASSES, CHUNK, PACK], BF16, tag="grouped", name="grouped%d" % c, align_bytes=64)
             if c == 0:
+                new_codes(c)
                 for g in range(PASSES):
                     regroup_by_vector(c, slice(g, g + 1), CHUNK)
+                    quantise_passes(c, slice(g, g + 1))
                 return
             regroup_by_vector(c, slice(0, PASSES), VECTOR_PIXELS)
             start = VECTOR_PIXELS - OVERLAP
@@ -142,13 +144,19 @@ def tile_pam_module_pa_kernel(
                 op1=ADD,
             )
 
-        def quantise_chunk(c):
+        def new_codes(c):
             x_codes[c] = keep.tile([P, PASSES, CHUNK], U32, name="x_codes%d" % c, align_bytes=64)
             x_scales[c] = keep.tile([P, PASSES, CHUNK], U8, name="x_scales%d" % c, align_bytes=64)
+
+        def quantise_chunk(c):
+            new_codes(c)
+            quantise_passes(c, slice(0, PASSES))
+
+        def quantise_passes(c, passes):
             nc.vector.quantize_mx(
-                out=x_codes[c][:].rearrange("p g w -> p (g w)").bitcast(FP8X4),
-                scales=x_scales[c][:].rearrange("p g w -> p (g w)"),
-                in_=grouped[c][:].rearrange("p g w t -> p (g w t)"),
+                out=x_codes[c][:, passes].rearrange("p g w -> p (g w)").bitcast(FP8X4),
+                scales=x_scales[c][:, passes].rearrange("p g w -> p (g w)"),
+                in_=grouped[c][:, passes].rearrange("p g w t -> p (g w t)"),
             )
 
         row_sum = keep.tile([P, BATCH, TILES, HEIGHT], F32)
@@ -159,17 +167,20 @@ def tile_pam_module_pa_kernel(
         column_bank = {}
         map_sum = {}
 
+        def one_pass(out, c, m, g, first, width, start, stop):
+            nc.tensor.matmul_mx(
+                out=out,
+                lhsT=w_codes[:, g, P * m : P * (m + 1)].bitcast(FP8X4),
+                lhsT_scale=w_scales[:, g, P * m : P * (m + 1)],
+                rhs=x_codes[c][:, g, first : first + width].bitcast(FP8X4),
+                rhs_scale=x_scales[c][:, g, first : first + width],
+                start=start,
+                stop=stop,
+            )
+
         def multiply(out, c, m, first, width, start, stop):
             for g in range(PASSES):
-                nc.tensor.matmul_mx(
-                    out=out,
-                    lhsT=w_codes[:, g, P * m : P * (m + 1)].bitcast(FP8X4),
-                    lhsT_scale=w_scales[:, g, P * m : P * (m + 1)],
-                    rhs=x_codes[c][:, g, first : first + width].bitcast(FP8X4),
-                    rhs_scale=x_scales[c][:, g, first : first + width],
-                    start=start and g == 0,
-                    stop=stop and g == PASSES - 1,
-                )
+                one_pass(out, c, m, g, first, width, start and g == 0, stop and g == PASSES - 1)
 
         def sum_over_rows(out, some_rows):
             nc.vector.tensor_reduce(out=out, in_=some_rows.rearrange("p i j -> p j i"), axis=AXIS_X, op=ADD)
@@ -221,7 +232,15 @@ def tile_pam_module_pa_kernel(
             return [lambda: add_chunks_up(n, first_column_tile, middle), lambda: add_chunks_up(n, middle, TILES)]
 
         regroup_chunk(0)
-        quantise_chunk(0)
+        head_start = {}
+        for m in first_half:
+            if len(head_start) < PSUM_BANKS - TENSOR_GROUP:
+                head_start[m] = banks.tile([P, CHUNK], F32, tag="bank", name="head_start%d" % m)
+            else:
+                head_start[m] = column_banks.tile([P, CHUNK], F32, tag="column_bank", name="head_start%d" % m)
+        for g in range(PASSES):
+            for m in first_half:
+                one_pass(head_start[m][:], 0, m, g, 0, CHUNK, g == 0, g == PASSES - 1)
         regroup_chunk(1)
         waiting = []
         for c in range(ALL_CHUNKS):
@@ -248,8 +267,11 @@ def tile_pam_module_pa_kernel(
                         for step in closing_steps(n):
                             step()
                         store_means(n, first_column_tile, TILES)
-                bank = banks.tile([P, CHUNK], F32, tag="bank")
-                multiply(bank[:], c, m, 0, CHUNK, True, True)
+                if c == 0 and m in head_start:
+                    bank = head_start[m]
+                else:
+                    bank = banks.tile([P, CHUNK], F32, tag="bank")
+                    multiply(bank[:], c, m, 0, CHUNK, True, True)
                 by_row = bank[:].rearrange("p (i j) -> p i j", j=WIDTH)
                 if m in vector_tiles:
                     sum_along_rows(row_sum[:, n, m, rows], by_row)

@@ -12,6 +12,7 @@ FP8X4 = mybir.dt.float8_e4m3fn_x4
 ADD = mybir.AluOpType.add
 MULT = mybir.AluOpType.mult
 AXIS_X = mybir.AxisListType.X
+AXIS_XY = mybir.AxisListType.XY
 COPY = mybir.ActivationFunctionType.Copy
 
 P = 128
@@ -24,20 +25,19 @@ CHUNK = 512
 ROWS = CHUNK // WIDTH
 CHUNKS = PIXELS // CHUNK
 ALL_CHUNKS = BATCH * CHUNKS
+BLOCKS = 4
+BLOCK_WIDTH = WIDTH // BLOCKS
+WINDOW = ROWS * BLOCK_WIDTH
 OUT_Q, OUT_K, OUT_V = 128, 128, 1024
 OUT_ALL = OUT_Q + OUT_K + OUT_V
 TILES = OUT_ALL // P
-PSUM_BANKS = 8
 
-TENSOR_GROUP = 4
-GPSIMD_GROUP = 2
-SHARED_GROUP = 1
-VECTOR_GROUP = TILES - TENSOR_GROUP - GPSIMD_GROUP - SHARED_GROUP
-SCALAR_ROWS = 6
-FOLD = 256
-
-VECTOR_PIXELS = 256
-OVERLAP = 4
+TWICE_TILES = [7, 8, 9]
+GPSIMD_TILE = 2
+SHARED_TILES = [3, 4, 5, 6, 0, 1]
+ONCE_TILES = [GPSIMD_TILE] + SHARED_TILES
+ONCE = len(ONCE_TILES)
+FREE_BANKS = 4
 
 FLOPS = 2 * OUT_ALL * CHANNELS * BATCH * PIXELS
 
@@ -46,37 +46,35 @@ def tile_pam_module_pa_kernel(
     tc, x, Wq_words, Wq_scales, bq, Wk_words, Wk_scales, bk, Wv_words, Wv_scales, bv, out_0, out_1, out_2
 ):
     nc = tc.nc
-    tensor_tiles = list(range(TENSOR_GROUP))
-    gpsimd_tiles = list(range(TENSOR_GROUP, TENSOR_GROUP + GPSIMD_GROUP))
-    shared_tiles = list(range(TENSOR_GROUP + GPSIMD_GROUP, TILES - VECTOR_GROUP))
-    vector_tiles = list(range(TILES - VECTOR_GROUP, TILES))
-    first_column_tile = shared_tiles[0]
-    scalar_first_half = gpsimd_tiles + shared_tiles
-    first_half = [group[r] for r in range(TILES) for group in (vector_tiles, scalar_first_half) if r < len(group)]
-    tile_order = first_half + tensor_tiles
+    twice = len(TWICE_TILES)
 
     with ExitStack() as ctx:
         keep = ctx.enter_context(tc.tile_pool(name="keep", bufs=1))
-        stage = ctx.enter_context(tc.tile_pool(name="stage", bufs=1))
+        stage = ctx.enter_context(tc.tile_pool(name="stage", bufs=3))
         products = ctx.enter_context(tc.tile_pool(name="products", bufs=6))
-        banks = ctx.enter_context(tc.psum_pool(name="banks", bufs=PSUM_BANKS - TENSOR_GROUP))
-        column_banks = ctx.enter_context(tc.psum_pool(name="column_banks", bufs=TENSOR_GROUP))
+        banks = ctx.enter_context(tc.psum_pool(name="banks", bufs=FREE_BANKS))
+        row_banks = ctx.enter_context(tc.psum_pool(name="row_banks", bufs=1))
+        column_banks = ctx.enter_context(tc.psum_pool(name="column_banks", bufs=twice))
         ctx.enter_context(tc.manual_schedule())
 
         x_view = x.rearrange("n (g p t) h w -> n g p t (h w)", g=PASSES, p=P, t=PACK)
         raw = {}
 
-        def load_chunk(c):
+        def load_half(c, g):
             n, part = divmod(c, CHUNKS)
-            raw[c] = keep.tile([P, PASSES, PACK, CHUNK], BF16, name="raw%d" % c)
-            for g in range(PASSES):
-                nc.sync.dma_start(out=raw[c][:, g], in_=x_view[n, g, :, :, CHUNK * part : CHUNK * (part + 1)])
+            if g == 0:
+                raw[c] = keep.tile([P, PASSES, PACK, CHUNK], BF16, name="raw%d" % c)
+            nc.sync.dma_start(out=raw[c][:, g], in_=x_view[n, g, :, :, CHUNK * part : CHUNK * (part + 1)])
 
-        load_chunk(0)
+        def load_chunk(c):
+            for g in range(PASSES):
+                load_half(c, g)
+
+        load_half(0, 0)
 
         w_codes = keep.tile([P, PASSES, OUT_ALL], U32, align_bytes=64)
         w_scales = keep.tile([P, PASSES, OUT_ALL], U8, align_bytes=64)
-        nc.gpsimd.memset(w_scales[:].bitcast(F32), 0.0)
+        nc.vector.memset(w_scales[:].bitcast(I32), 0)
 
         def load_scales(scales, first, width):
             scale_rows = scales.rearrange("g q n -> q g n")
@@ -86,86 +84,80 @@ def tile_pam_module_pa_kernel(
                     in_=scale_rows[4 * quadrant : 4 * quadrant + 4].bitcast(I32),
                 )
 
-        def load_words(words, first, start, stop):
+        def load_words(words, g, first, width):
             nc.sync.dma_start(
-                out=w_codes[:, :, first + start : first + stop].bitcast(I32),
-                in_=words[:, :, start:stop, :].rearrange("g p n t -> p g (n t)").bitcast(I32),
+                out=w_codes[:, g, first : first + width].bitcast(I32),
+                in_=words[g].rearrange("p n t -> p (n t)").bitcast(I32),
             )
 
         first_v = OUT_Q + OUT_K
-        v_of_tensor_group = P * TENSOR_GROUP - first_v
         load_scales(Wv_scales, first_v, OUT_V)
-        load_words(Wv_words, first_v, v_of_tensor_group, OUT_V)
+        load_words(Wv_words, 0, first_v, OUT_V)
+        load_half(0, 1)
+        load_words(Wv_words, 1, first_v, OUT_V)
         load_chunk(1)
-        load_words(Wq_words, 0, 0, OUT_Q)
         load_scales(Wq_scales, 0, OUT_Q)
-        load_words(Wk_words, OUT_Q, 0, OUT_K)
         load_scales(Wk_scales, OUT_Q, OUT_K)
-        load_words(Wv_words, first_v, 0, v_of_tensor_group)
-        load_chunk(2)
+        for g in range(PASSES):
+            load_words(Wq_words, g, 0, OUT_Q)
+            load_words(Wk_words, g, OUT_Q, OUT_K)
 
         bias_rows = keep.tile([P, P], BF16)
-        nc.gpsimd.memset(bias_rows[:], 0.0)
+        nc.vector.memset(bias_rows[:], 0.0)
         nc.sync.dma_start(out=bias_rows[0:1, :], in_=bq.rearrange("(m p) -> m p", p=P))
         nc.sync.dma_start(out=bias_rows[1:2, :], in_=bk.rearrange("(m p) -> m p", p=P))
         nc.sync.dma_start(out=bias_rows[2:TILES, :], in_=bv.rearrange("(m p) -> m p", p=P))
-        identity = keep.tile([P, P], BF16)
-        make_identity(nc, identity[:])
-
-        for c in range(3, ALL_CHUNKS):
+        for c in range(2, ALL_CHUNKS):
             load_chunk(c)
 
         grouped = {}
         x_codes = {}
         x_scales = {}
 
-        def regroup_by_vector(c, passes, stop):
-            nc.vector.tensor_copy(
-                out=grouped[c][:, passes, 0:stop, :].rearrange("p g (w i) t -> p g w t i", i=4),
-                in_=raw[c][:, passes, :, 0:stop].rearrange("p g t (w i) -> p g w t i", i=4),
-            )
-
-        def regroup_chunk(c):
+        def new_grouped(c):
             grouped[c] = stage.tile([P, PASSES, CHUNK, PACK], BF16, tag="grouped", name="grouped%d" % c, align_bytes=64)
-            if c == 0:
-                new_codes(c)
-                for g in range(PASSES):
-                    regroup_by_vector(c, slice(g, g + 1), CHUNK)
-                    quantise_passes(c, slice(g, g + 1))
-                return
-            regroup_by_vector(c, slice(0, PASSES), VECTOR_PIXELS)
-            start = VECTOR_PIXELS - OVERLAP
-            nc.gpsimd.tensor_scalar(
-                out=grouped[c][:, :, start:, :],
-                in0=raw[c][:, :, :, start:].rearrange("p g t w -> p g w t"),
-                scalar1=1.0,
-                scalar2=0.0,
-                op0=MULT,
-                op1=ADD,
+
+        def piece_of(c, g, b):
+            target = grouped[c][:, g, WINDOW * b : WINDOW * (b + 1), :].rearrange("p (r w) t -> p r w t", w=BLOCK_WIDTH)
+            source = raw[c][:, g].rearrange("p t (r w) -> p r w t", w=WIDTH)[:, :, BLOCK_WIDTH * b : BLOCK_WIDTH * (b + 1), :]
+            return target, source
+
+        def vector_piece(c, g, b):
+            target, source = piece_of(c, g, b)
+            nc.vector.tensor_copy(
+                out=target.rearrange("p r (v i) t -> p r v t i", i=4), in_=source.rearrange("p r (v i) t -> p r v t i", i=4)
             )
 
-        def new_codes(c):
-            x_codes[c] = keep.tile([P, PASSES, CHUNK], U32, name="x_codes%d" % c, align_bytes=64)
-            x_scales[c] = keep.tile([P, PASSES, CHUNK], U8, name="x_scales%d" % c, align_bytes=64)
+        def vector_pieces(c, g):
+            vector_piece(c, g, 0)
+            vector_piece(c, g, 1)
 
-        def quantise_chunk(c):
-            new_codes(c)
-            quantise_passes(c, slice(0, PASSES))
+        def gpsimd_piece(c, g, b):
+            target, source = piece_of(c, g, b)
+            nc.gpsimd.tensor_scalar(out=target, in0=source, scalar1=1.0, scalar2=0.0, op0=MULT, op1=ADD)
 
-        def quantise_passes(c, passes):
+        def scalar_piece(c, g, b):
+            target, source = piece_of(c, g, b)
+            nc.scalar.copy(out=target, in_=source)
+
+        def quantise_half(c, g):
+            if g == 0:
+                x_codes[c] = keep.tile([P, PASSES, CHUNK], U32, name="x_codes%d" % c, align_bytes=64)
+                x_scales[c] = keep.tile([P, PASSES, CHUNK], U8, name="x_scales%d" % c, align_bytes=64)
             nc.vector.quantize_mx(
-                out=x_codes[c][:, passes].rearrange("p g w -> p (g w)").bitcast(FP8X4),
-                scales=x_scales[c][:, passes].rearrange("p g w -> p (g w)"),
-                in_=grouped[c][:, passes].rearrange("p g w t -> p (g w t)"),
+                out=x_codes[c][:, g].bitcast(FP8X4),
+                scales=x_scales[c][:, g],
+                in_=grouped[c][:, g].rearrange("p w t -> p (w t)"),
             )
 
         row_sum = keep.tile([P, BATCH, TILES, HEIGHT], F32)
-        col_part = keep.tile([P, BATCH, TILES, CHUNKS, WIDTH], F32)
+        col_part = keep.tile([P, BATCH, ONCE, CHUNKS, WIDTH], F32)
         col_sum = keep.tile([P, BATCH, TILES, WIDTH], F32)
         pooled = keep.tile([P, BATCH, TILES, HEIGHT + WIDTH], F32)
         bias = keep.tile([P, TILES], F32)
-        column_bank = {}
+        early = keep.tile([P, ONCE, WIDTH], F32)
         map_sum = {}
+        nc.vector.memset(col_part[:, :, GPSIMD_TILE, 0 : CHUNKS - 1, :], 0.0)
 
         def one_pass(out, c, m, g, first, width, start, stop):
             nc.tensor.matmul_mx(
@@ -178,33 +170,140 @@ def tile_pam_module_pa_kernel(
                 stop=stop,
             )
 
-        def multiply(out, c, m, first, width, start, stop):
-            for g in range(PASSES):
-                one_pass(out, c, m, g, first, width, start and g == 0, stop and g == PASSES - 1)
+        once_bank = {}
+        row_bank = {}
+        column_bank = {}
 
-        def sum_over_rows(out, some_rows):
-            nc.vector.tensor_reduce(out=out, in_=some_rows.rearrange("p i j -> p j i"), axis=AXIS_X, op=ADD)
+        def once_pass(c, m, g):
+            if g == 0:
+                once_bank[m] = banks.tile([P, CHUNK], F32, tag="bank", name="bank%d_%d" % (c, m))
+            one_pass(once_bank[m][:], c, m, g, 0, CHUNK, g == 0, g == PASSES - 1)
 
-        def sum_along_rows(out, some_rows):
-            nc.vector.tensor_reduce(out=out, in_=some_rows, axis=AXIS_X, op=ADD)
-
-        def store_means(n, lo, hi):
-            nc.vector.scalar_tensor_tensor(
-                out=pooled[:, n, lo:hi, 0:HEIGHT],
-                in0=row_sum[:, n, lo:hi, :],
-                scalar=1.0 / WIDTH,
-                in1=bias[:, lo:hi].unsqueeze(2).to_broadcast([P, hi - lo, HEIGHT]),
-                op0=MULT,
-                op1=ADD,
+        def column_pass(c, m, g):
+            part = c % CHUNKS
+            if part == 0 and g == 0:
+                column_bank[m] = column_banks.tile([P, CHUNK], F32, tag="column_bank", name="column_bank%d_%d" % (c, m))
+            one_pass(
+                column_bank[m][:], c, m, g, 0, CHUNK, part == 0 and g == 0, part == CHUNKS - 1 and g == PASSES - 1
             )
+
+        def row_passes(c, m):
+            k = TWICE_TILES.index(m)
+            if k == 0:
+                row_bank[0] = row_banks.tile([P, CHUNK // WINDOW, WINDOW], F32, tag="row_bank", name="row_bank%d" % c)
+            for g in range(PASSES):
+                for b in range(BLOCKS):
+                    one_pass(
+                        row_bank[0][:, k], c, m, g, WINDOW * b, WINDOW, g == 0 and b == 0, g == PASSES - 1 and b == BLOCKS - 1
+                    )
+
+        def tensor_step(c, kind, m):
+            if kind == "row":
+                row_passes(c, m)
+                return
+            for g in range(PASSES):
+                if kind == "once":
+                    once_pass(c, m, g)
+                else:
+                    column_pass(c, m, g)
+
+        def sum_columns(out, bank):
+            nc.vector.tensor_reduce(
+                out=out.rearrange("p (b w) -> p b w", w=BLOCK_WIDTH),
+                in_=bank.rearrange("p (b r w) -> p b w r", b=BLOCKS, w=BLOCK_WIDTH),
+                axis=AXIS_X,
+                op=ADD,
+            )
+
+        def sum_rows(out, bank):
+            nc.vector.tensor_reduce(
+                out=out, in_=bank.rearrange("p (b r w) -> p r b w", b=BLOCKS, w=BLOCK_WIDTH), axis=AXIS_XY, op=ADD
+            )
+
+        def scalar_rows(c, m):
+            n, part = divmod(c, CHUNKS)
+            by_row = once_bank[m][:].rearrange("p (b r w) -> p r b w", b=BLOCKS, w=BLOCK_WIDTH)
+            if m == GPSIMD_TILE and part == 0:
+                map_sum[n] = keep.tile([P, ROWS, WIDTH], F32, name="map_sum%d" % n)
+                product = map_sum[n]
+            else:
+                product = products.tile([P, ROWS, WIDTH], F32, tag="product", name="product%d_%d" % (c, m))
+            for i in range(ROWS):
+                nc.scalar.activation(
+                    out=product[:, i, :].rearrange("p (b w) -> p b w", w=BLOCK_WIDTH),
+                    in_=by_row[:, i],
+                    func=COPY,
+                    accum_out=row_sum[:, n, m, ROWS * part + i : ROWS * part + i + 1],
+                )
+            return product
+
+        def gpsimd_sum(c, product):
+            n, part = divmod(c, CHUNKS)
+            so_far = map_sum[n]
+            if part > 0:
+                nc.gpsimd.tensor_tensor(out=so_far[:], in0=so_far[:], in1=product[:], op=ADD)
+            if part == CHUNKS - 1:
+                for half in (ROWS // 2, ROWS // 4):
+                    nc.gpsimd.tensor_tensor(
+                        out=so_far[:, 0:half, :], in0=so_far[:, 0:half, :], in1=so_far[:, half : 2 * half, :], op=ADD
+                    )
+                nc.gpsimd.tensor_tensor(
+                    out=col_part[:, n, GPSIMD_TILE, CHUNKS - 1, :], in0=so_far[:, 0, :], in1=so_far[:, 1, :], op=ADD
+                )
+
+        def vector_columns(c, m):
+            n, part = divmod(c, CHUNKS)
+            sum_columns(col_part[:, n, m, part, :], once_bank[m][:])
+
+        def vector_rows(c, lo, hi):
+            n, part = divmod(c, CHUNKS)
+            nc.vector.tensor_reduce(
+                out=row_sum[:, n, TWICE_TILES[0] + lo : TWICE_TILES[0] + hi, ROWS * part : ROWS * (part + 1)],
+                in_=row_bank[0][:, lo:hi].rearrange("p m (r w) -> p m r w", w=BLOCK_WIDTH),
+                axis=AXIS_X,
+                op=ADD,
+            )
+
+        def add_parts(n, lo, hi):
+            nc.vector.tensor_reduce(
+                out=col_sum[:, n, lo:hi, :], in_=col_part[:, n, lo:hi].rearrange("p m c j -> p m j c"), axis=AXIS_X, op=ADD
+            )
+
+        def add_early_parts(n, lo, hi):
+            nc.vector.tensor_reduce(
+                out=early[:, lo:hi, :], in_=col_part[:, n, lo:hi, 0 : CHUNKS - 1].rearrange("p m c j -> p m j c"), axis=AXIS_X, op=ADD
+            )
+
+        def early_column_means(lo, hi):
+            mean(early[:, lo:hi, :], early[:, lo:hi, :], lo, hi, WIDTH, HEIGHT)
+
+        def late_column_means(n, lo, hi):
             nc.vector.scalar_tensor_tensor(
                 out=pooled[:, n, lo:hi, HEIGHT:],
-                in0=col_sum[:, n, lo:hi, :],
+                in0=col_part[:, n, lo:hi, CHUNKS - 1, :],
                 scalar=1.0 / HEIGHT,
-                in1=bias[:, lo:hi].unsqueeze(2).to_broadcast([P, hi - lo, WIDTH]),
+                in1=early[:, lo:hi, :],
                 op0=MULT,
                 op1=ADD,
             )
+
+        def mean(out, sums, lo, hi, length, count):
+            nc.vector.scalar_tensor_tensor(
+                out=out,
+                in0=sums,
+                scalar=1.0 / count,
+                in1=bias[:, lo:hi].unsqueeze(2).to_broadcast([P, hi - lo, length]),
+                op0=MULT,
+                op1=ADD,
+            )
+
+        def row_means(n, lo, hi):
+            mean(pooled[:, n, lo:hi, 0:HEIGHT], row_sum[:, n, lo:hi, :], lo, hi, HEIGHT, WIDTH)
+
+        def column_means(n, lo, hi):
+            mean(pooled[:, n, lo:hi, HEIGHT:], col_sum[:, n, lo:hi, :], lo, hi, WIDTH, HEIGHT)
+
+        def store(n, lo, hi):
             if lo == 0:
                 nc.sync.dma_start(out=out_0[n], in_=pooled[:, n, 0, :])
                 nc.sync.dma_start(out=out_1[n], in_=pooled[:, n, 1, :])
@@ -213,119 +312,128 @@ def tile_pam_module_pa_kernel(
                 out=out_2[n].rearrange("(m p) f -> p m f", p=P)[:, first - 2 : hi - 2, :], in_=pooled[:, n, first:hi, :]
             )
 
-        def fold_map_sum(n):
-            for half in (ROWS // 2, ROWS // 4):
-                nc.gpsimd.tensor_tensor(
-                    out=map_sum[n][:, :, 0:half, :], in0=map_sum[n][:, :, 0:half, :], in1=map_sum[n][:, :, half : 2 * half, :], op=ADD
-                )
-            nc.gpsimd.tensor_tensor(
-                out=col_sum[:, n, gpsimd_tiles[0] : first_column_tile, :], in0=map_sum[n][:, :, 0, :], in1=map_sum[n][:, :, 1, :], op=ADD
-            )
-
-        def add_chunks_up(n, lo, hi):
-            nc.vector.tensor_reduce(
-                out=col_sum[:, n, lo:hi, :], in_=col_part[:, n, lo:hi, :, :].rearrange("p m c j -> p m j c"), axis=AXIS_X, op=ADD
-            )
-
-        def closing_steps(n):
-            middle = (first_column_tile + TILES) // 2
-            return [lambda: add_chunks_up(n, first_column_tile, middle), lambda: add_chunks_up(n, middle, TILES)]
-
-        regroup_chunk(0)
-        head_start = {}
-        for m in first_half:
-            if len(head_start) < PSUM_BANKS - TENSOR_GROUP:
-                head_start[m] = banks.tile([P, CHUNK], F32, tag="bank", name="head_start%d" % m)
-            else:
-                head_start[m] = column_banks.tile([P, CHUNK], F32, tag="column_bank", name="head_start%d" % m)
+        new_grouped(0)
         for g in range(PASSES):
-            for m in first_half:
-                one_pass(head_start[m][:], 0, m, g, 0, CHUNK, g == 0, g == PASSES - 1)
-        regroup_chunk(1)
-        waiting = []
+            gpsimd_piece(0, g, 2)
+            scalar_piece(0, g, 3)
+            vector_piece(0, g, 0)
+            vector_piece(0, g, 1)
+            quantise_half(0, g)
+        identity = keep.tile([P, P], BF16)
+        make_identity(nc, identity[:])
+        new_grouped(1)
+        for g in range(PASSES):
+            gpsimd_piece(1, g, 2)
+            gpsimd_piece(1, g, 3)
+
+        row_steps = [("row", m) for m in TWICE_TILES]
+        column_steps = [("column", m) for m in TWICE_TILES]
+        between = [step for pair in zip(row_steps, column_steps) for step in pair]
+        usual_order = []
+        for k, m in enumerate(ONCE_TILES):
+            usual_order.append(("once", m))
+            if k < len(between):
+                usual_order.append(between[k])
+        ahead = ONCE_TILES[:FREE_BANKS]
+        first_order = [("once", m) for m in ahead] + column_steps
+        for k, m in enumerate(ONCE_TILES[FREE_BANKS:]):
+            first_order += [row_steps[k], ("once", m)]
+        last_order = [step for step in usual_order if step != row_steps[-1] and step != column_steps[-1]]
+        last_order += [column_steps[-1], row_steps[-1]]
+
+        for m in ahead:
+            once_pass(0, m, 0)
+        for m in TWICE_TILES:
+            column_pass(0, m, 0)
+
+        closing = {
+            CHUNKS + 1: [lambda: add_parts(0, 0, 4)],
+            CHUNKS + 2: [
+                lambda: add_parts(0, 4, ONCE),
+                lambda: column_means(0, 0, TILES),
+                lambda: row_means(0, 0, TILES),
+                lambda: store(0, 0, TILES),
+            ],
+            ALL_CHUNKS - 1: [
+                lambda: add_early_parts(BATCH - 1, 0, 4),
+                lambda: add_early_parts(BATCH - 1, 4, ONCE),
+                lambda: early_column_means(0, ONCE),
+            ],
+        }
+        pending = []
         for c in range(ALL_CHUNKS):
             n, part = divmod(c, CHUNKS)
-            rows = slice(ROWS * part, ROWS * (part + 1))
-            last_of_map = part == CHUNKS - 1
-            last_of_all = c == ALL_CHUNKS - 1
-            after_scalar = []
-            for m in tile_order:
-                if m == tensor_tiles[0]:
-                    if waiting:
-                        waiting.pop(0)()
-                    for read in after_scalar:
-                        read()
-                    if not last_of_all:
-                        quantise_chunk(c + 1)
-                    if c + 2 < ALL_CHUNKS:
-                        regroup_chunk(c + 2)
-                    else:
-                        for step in waiting:
-                            step()
-                        waiting = []
-                    if last_of_all:
-                        for step in closing_steps(n):
-                            step()
-                        store_means(n, first_column_tile, TILES)
-                if c == 0 and m in head_start:
-                    bank = head_start[m]
-                else:
-                    bank = banks.tile([P, CHUNK], F32, tag="bank")
-                    multiply(bank[:], c, m, 0, CHUNK, True, True)
-                by_row = bank[:].rearrange("p (i j) -> p i j", j=WIDTH)
-                if m in vector_tiles:
-                    sum_along_rows(row_sum[:, n, m, rows], by_row)
-                    sum_over_rows(col_part[:, n, m, part, :], by_row)
-                    continue
-                if m in gpsimd_tiles and part == 0:
-                    if m == gpsimd_tiles[0]:
-                        map_sum[n] = keep.tile([P, GPSIMD_GROUP, ROWS, WIDTH], F32, name="map_sum%d" % n)
-                    product = map_sum[n][:, m - gpsimd_tiles[0]]
-                else:
-                    product_tile = products.tile([P, ROWS, WIDTH], F32, tag="product")
-                    product = product_tile[:]
-                very_last = last_of_all and m == tile_order[-1]
-                scalar_rows = SCALAR_ROWS if m in shared_tiles else 0 if very_last else ROWS
-                if very_last:
-                    sum_along_rows(row_sum[:, n, m, rows], by_row)
-                for i in range(scalar_rows):
-                    nc.scalar.activation(
-                        out=product[:, i, :],
-                        in_=by_row[:, i, :],
-                        func=COPY,
-                        accum_out=row_sum[:, n, m, ROWS * part + i : ROWS * part + i + 1],
-                    )
-                if m in shared_tiles:
-                    after_scalar.append(
-                        lambda m=m, by_row=by_row: sum_along_rows(
-                            row_sum[:, n, m, ROWS * part + SCALAR_ROWS : ROWS * (part + 1)], by_row[:, SCALAR_ROWS:, :]
-                        )
-                    )
-                    after_scalar.append(lambda m=m, by_row=by_row: sum_over_rows(col_part[:, n, m, part, :], by_row))
-                elif m in gpsimd_tiles:
-                    if part > 0:
-                        so_far = map_sum[n][:, m - gpsimd_tiles[0]]
-                        nc.gpsimd.tensor_tensor(out=so_far, in0=so_far, in1=product, op=ADD)
-                    if m == gpsimd_tiles[-1]:
-                        if part == 0 and n > 0:
-                            fold_map_sum(n - 1)
-                        if last_of_all:
-                            fold_map_sum(n)
-                else:
-                    if part == 0:
-                        column_bank[m] = column_banks.tile([P, FOLD], F32, tag="column_bank", name="column_bank%d_%d" % (n, m))
-                    for first in range(0, CHUNK, FOLD):
-                        multiply(column_bank[m][:], c, m, first, FOLD, part == 0 and first == 0, last_of_map and first == CHUNK - FOLD)
-                    if last_of_map:
-                        sum_over_rows(col_sum[:, n, m, :], column_bank[m][:].rearrange("p (i j) -> p i j", j=WIDTH))
+            last = c == ALL_CHUNKS - 1
+            order = first_order if c == 0 else last_order if last else usual_order
+            extra = []
+            copies = c + 2 < ALL_CHUNKS
+            if copies:
+                new_grouped(c + 2)
+                gpsimd_piece(c + 2, 0, 2)
+                gpsimd_piece(c + 2, 0, 3)
             if c == 0:
-                bias_bank = banks.tile([P, P], BF16, tag="bank")
+                extra = [lambda: None, lambda: None]
+                extra += [lambda g=g: vector_pieces(1, g) for g in range(PASSES)]
+                extra += [lambda g=g: quantise_half(1, g) for g in range(PASSES)]
+                extra += [lambda g=g: vector_pieces(2, g) for g in range(PASSES)]
+            else:
+                for g in range(PASSES):
+                    if copies:
+                        extra.append(lambda g=g: vector_piece(c + 2, g, 0))
+                    if not last:
+                        extra.append(lambda g=g: quantise_half(c + 1, g))
+                if copies:
+                    extra += [lambda g=g: vector_piece(c + 2, g, 1) for g in range(PASSES)]
+            extra += closing.get(c, [])
+            done_once = 0
+            done_rows = 0
+            for kind, m in order:
+                if c == 0 and (m in ahead or kind == "column"):
+                    if kind == "once":
+                        one_pass(once_bank[m][:], c, m, 1, 0, CHUNK, False, True)
+                    else:
+                        column_pass(c, m, 1)
+                else:
+                    tensor_step(c, kind, m)
+                if kind == "row":
+                    done_rows += 1
+                    if last and done_rows == twice - 1:
+                        pending.append(lambda: vector_rows(c, 0, twice - 1))
+                    elif done_rows == twice and not last:
+                        pending.append(lambda: vector_rows(c, 0, twice))
+                if kind == "column" and part == CHUNKS - 1:
+                    pending.append(lambda m=m: sum_columns(col_sum[:, n, m, :], column_bank[m][:]))
+                if kind == "once":
+                    if last and m == ONCE_TILES[-1]:
+                        pending.append(lambda m=m: sum_rows(row_sum[:, n, m, ROWS * part :], once_bank[m][:]))
+                    else:
+                        product = scalar_rows(c, m)
+                    for read in pending:
+                        read()
+                    pending = []
+                    if m != GPSIMD_TILE:
+                        pending.append(lambda m=m, c=c: vector_columns(c, m))
+                    if extra:
+                        extra.pop(0)()
+                    if done_once == 0:
+                        gpsimd_sum(c, product)
+                        if copies:
+                            gpsimd_piece(c + 2, 1, 2)
+                            gpsimd_piece(c + 2, 1, 3)
+                    done_once += 1
+            for step in extra:
+                step()
+            if c == 0:
+                bias_bank = banks.tile([P, P], BF16, tag="bank", name="bias_bank")
                 nc.tensor.transpose(bias_bank[:], bias_rows[:], identity[:])
                 nc.vector.tensor_copy(out=bias[:], in_=bias_bank[:, 0:TILES])
-            if last_of_map:
-                if last_of_all:
-                    store_means(n, TENSOR_GROUP, first_column_tile)
-                    store_means(n, 0, TENSOR_GROUP)
-                else:
-                    waiting = [lambda n=n: store_means(n, 0, TENSOR_GROUP)] + closing_steps(n)
-                    waiting.append(lambda n=n: store_means(n, TENSOR_GROUP, TILES))
+        n = BATCH - 1
+        for read in pending:
+            read()
+        late_column_means(n, 0, ONCE)
+        row_means(n, 0, ONCE)
+        store(n, 0, ONCE)
+        vector_rows(ALL_CHUNKS - 1, twice - 1, twice)
+        column_means(n, ONCE, TILES)
+        row_means(n, ONCE, TILES)
+        store(n, ONCE, TILES)

@@ -14,6 +14,7 @@ MULT = mybir.AluOpType.mult
 AXIS_X = mybir.AxisListType.X
 AXIS_XY = mybir.AxisListType.XY
 COPY = mybir.ActivationFunctionType.Copy
+IDENTITY = mybir.ActivationFunctionType.Identity
 
 P = 128
 PACK = 4
@@ -38,6 +39,19 @@ SHARED_TILES = [3, 4, 5, 6, 0, 1]
 ONCE_TILES = [GPSIMD_TILE] + SHARED_TILES
 ONCE = len(ONCE_TILES)
 FREE_BANKS = 4
+VECTOR_PIECES = [(0, 0), (0, 1), (1, 0)]
+SCALAR_PIECES = [(1, 1)]
+GPSIMD_PIECES = [(0, 2), (0, 3), (1, 2), (1, 3)]
+VECTOR_SLOTS = [1, 1, 4]
+SCALAR_SLOTS = [3]
+GPSIMD_SLOTS = [0, 1, 4, 5]
+GPSIMD_ADD_SLOT = 3
+QUANTISE_SLOTS = [0, 3]
+USUAL_BETWEEN = [[("column", 0)], [("column", 1)], [("row", 0)], [("row", 1)], [("row", 2)], [("column", 2)]]
+LATE_SLOTS = [[0, 1], [0, 2]]
+LATE_QUANTISE_SLOTS = [[1, 2], [1, 4]]
+FOLD_SLOT = 4
+LATE_SCALAR = [0, 1]
 
 FLOPS = 2 * OUT_ALL * CHANNELS * BATCH * PIXELS
 
@@ -84,30 +98,32 @@ def tile_pam_module_pa_kernel(
                     in_=scale_rows[4 * quadrant : 4 * quadrant + 4].bitcast(I32),
                 )
 
-        def load_words(words, g, first, width):
+        def load_words(words, first, width, passes):
             nc.sync.dma_start(
-                out=w_codes[:, g, first : first + width].bitcast(I32),
-                in_=words[g].rearrange("p n t -> p (n t)").bitcast(I32),
+                out=w_codes[:, passes, first : first + width].bitcast(I32),
+                in_=words[passes].rearrange("g p n t -> p g (n t)").bitcast(I32),
             )
 
         first_v = OUT_Q + OUT_K
         load_scales(Wv_scales, first_v, OUT_V)
-        load_words(Wv_words, 0, first_v, OUT_V)
+        load_words(Wv_words, first_v, OUT_V, slice(0, 1))
         load_half(0, 1)
-        load_words(Wv_words, 1, first_v, OUT_V)
-        load_chunk(1)
+        load_words(Wv_words, first_v, OUT_V, slice(1, 2))
+        load_half(1, 0)
         load_scales(Wq_scales, 0, OUT_Q)
+        load_half(1, 1)
         load_scales(Wk_scales, OUT_Q, OUT_K)
-        for g in range(PASSES):
-            load_words(Wq_words, g, 0, OUT_Q)
-            load_words(Wk_words, g, OUT_Q, OUT_K)
+        load_words(Wq_words, 0, OUT_Q, slice(0, PASSES))
+        load_words(Wk_words, OUT_Q, OUT_K, slice(0, PASSES))
+        for c in range(2, CHUNKS):
+            load_chunk(c)
 
         bias_rows = keep.tile([P, P], BF16)
         nc.vector.memset(bias_rows[:], 0.0)
         nc.sync.dma_start(out=bias_rows[0:1, :], in_=bq.rearrange("(m p) -> m p", p=P))
         nc.sync.dma_start(out=bias_rows[1:2, :], in_=bk.rearrange("(m p) -> m p", p=P))
         nc.sync.dma_start(out=bias_rows[2:TILES, :], in_=bv.rearrange("(m p) -> m p", p=P))
-        for c in range(2, ALL_CHUNKS):
+        for c in range(CHUNKS, ALL_CHUNKS):
             load_chunk(c)
 
         grouped = {}
@@ -127,10 +143,6 @@ def tile_pam_module_pa_kernel(
             nc.vector.tensor_copy(
                 out=target.rearrange("p r (v i) t -> p r v t i", i=4), in_=source.rearrange("p r (v i) t -> p r v t i", i=4)
             )
-
-        def vector_pieces(c, g):
-            vector_piece(c, g, 0)
-            vector_piece(c, g, 1)
 
         def gpsimd_piece(c, g, b):
             target, source = piece_of(c, g, b)
@@ -269,13 +281,17 @@ def tile_pam_module_pa_kernel(
                 out=col_sum[:, n, lo:hi, :], in_=col_part[:, n, lo:hi].rearrange("p m c j -> p m j c"), axis=AXIS_X, op=ADD
             )
 
-        def add_early_parts(n, lo, hi):
-            nc.vector.tensor_reduce(
-                out=early[:, lo:hi, :], in_=col_part[:, n, lo:hi, 0 : CHUNKS - 1].rearrange("p m c j -> p m j c"), axis=AXIS_X, op=ADD
-            )
+        def add_two_parts(n):
+            nc.gpsimd.tensor_tensor(out=early[:], in0=col_part[:, n, :, 0, :], in1=col_part[:, n, :, 1, :], op=ADD)
 
-        def early_column_means(lo, hi):
-            mean(early[:, lo:hi, :], early[:, lo:hi, :], lo, hi, WIDTH, HEIGHT)
+        def add_third_part(n):
+            nc.gpsimd.tensor_tensor(out=early[:], in0=early[:], in1=col_part[:, n, :, 2, :], op=ADD)
+
+        def early_column_means():
+            for m in range(ONCE):
+                nc.gpsimd.tensor_scalar(
+                    out=early[:, m, :], in0=early[:, m, :], scalar1=1.0 / HEIGHT, scalar2=bias[:, m : m + 1], op0=MULT, op1=ADD
+                )
 
         def late_column_means(n, lo, hi):
             nc.vector.scalar_tensor_tensor(
@@ -297,6 +313,11 @@ def tile_pam_module_pa_kernel(
                 op1=ADD,
             )
 
+        def scalar_row_mean(n, m):
+            nc.scalar.activation(
+                out=pooled[:, n, m, 0:HEIGHT], in_=row_sum[:, n, m, :], func=IDENTITY, scale=1.0 / WIDTH, bias=bias[:, m : m + 1]
+            )
+
         def row_means(n, lo, hi):
             mean(pooled[:, n, lo:hi, 0:HEIGHT], row_sum[:, n, lo:hi, :], lo, hi, HEIGHT, WIDTH)
 
@@ -314,26 +335,22 @@ def tile_pam_module_pa_kernel(
 
         new_grouped(0)
         for g in range(PASSES):
-            gpsimd_piece(0, g, 2)
-            scalar_piece(0, g, 3)
-            vector_piece(0, g, 0)
-            vector_piece(0, g, 1)
+            scalar_piece(0, g, BLOCKS - 1)
+            for b in range(BLOCKS - 1):
+                vector_piece(0, g, b)
             quantise_half(0, g)
         identity = keep.tile([P, P], BF16)
         make_identity(nc, identity[:])
         new_grouped(1)
-        for g in range(PASSES):
-            gpsimd_piece(1, g, 2)
-            gpsimd_piece(1, g, 3)
 
         row_steps = [("row", m) for m in TWICE_TILES]
         column_steps = [("column", m) for m in TWICE_TILES]
-        between = [step for pair in zip(row_steps, column_steps) for step in pair]
+        between = USUAL_BETWEEN
         usual_order = []
         for k, m in enumerate(ONCE_TILES):
             usual_order.append(("once", m))
             if k < len(between):
-                usual_order.append(between[k])
+                usual_order += [(kind, TWICE_TILES[i]) for kind, i in between[k]]
         ahead = ONCE_TILES[:FREE_BANKS]
         first_order = [("once", m) for m in ahead] + column_steps
         for k, m in enumerate(ONCE_TILES[FREE_BANKS:]):
@@ -346,45 +363,48 @@ def tile_pam_module_pa_kernel(
         for m in TWICE_TILES:
             column_pass(0, m, 0)
 
-        closing = {
-            CHUNKS + 1: [lambda: add_parts(0, 0, 4)],
-            CHUNKS + 2: [
-                lambda: add_parts(0, 4, ONCE),
-                lambda: column_means(0, 0, TILES),
-                lambda: row_means(0, 0, TILES),
-                lambda: store(0, 0, TILES),
-            ],
-            ALL_CHUNKS - 1: [
-                lambda: add_early_parts(BATCH - 1, 0, 4),
-                lambda: add_early_parts(BATCH - 1, 4, ONCE),
-                lambda: early_column_means(0, ONCE),
-            ],
-        }
         pending = []
         for c in range(ALL_CHUNKS):
             n, part = divmod(c, CHUNKS)
             last = c == ALL_CHUNKS - 1
             order = first_order if c == 0 else last_order if last else usual_order
-            extra = []
             copies = c + 2 < ALL_CHUNKS
+            vector_extra = [[] for k in range(ONCE)]
+            scalar_extra = [[] for k in range(ONCE)]
+            gpsimd_extra = [[] for k in range(ONCE)]
             if copies:
                 new_grouped(c + 2)
-                gpsimd_piece(c + 2, 0, 2)
-                gpsimd_piece(c + 2, 0, 3)
-            if c == 0:
-                extra = [lambda: None, lambda: None]
-                extra += [lambda g=g: vector_pieces(1, g) for g in range(PASSES)]
-                extra += [lambda g=g: quantise_half(1, g) for g in range(PASSES)]
-                extra += [lambda g=g: vector_pieces(2, g) for g in range(PASSES)]
-            else:
+                for (g, b), k in zip(GPSIMD_PIECES, GPSIMD_SLOTS):
+                    gpsimd_extra[k].append(lambda g=g, b=b: gpsimd_piece(c + 2, g, b))
+                for (g, b), k in zip(SCALAR_PIECES, SCALAR_SLOTS):
+                    scalar_extra[ONCE - 1 if c == 0 else k].append(lambda g=g, b=b: scalar_piece(c + 2, g, b))
+            gpsimd_extra[GPSIMD_ADD_SLOT].append(lambda: gpsimd_sum(c, gpsimd_product[0]))
+            if c < 2:
                 for g in range(PASSES):
-                    if copies:
-                        extra.append(lambda g=g: vector_piece(c + 2, g, 0))
-                    if not last:
-                        extra.append(lambda g=g: quantise_half(c + 1, g))
-                if copies:
-                    extra += [lambda g=g: vector_piece(c + 2, g, 1) for g in range(PASSES)]
-            extra += closing.get(c, [])
+                    if c == 0:
+                        scalar_extra[LATE_SCALAR[g]].append(lambda g=g: scalar_piece(1, g, BLOCKS - 1))
+                    for b in range(BLOCKS - 1):
+                        if c == 0 or (g, b) in VECTOR_PIECES:
+                            vector_extra[LATE_SLOTS[c][g]].append(lambda g=g, b=b: vector_piece(c + 1, g, b))
+                    vector_extra[LATE_QUANTISE_SLOTS[c][g]].append(lambda g=g: quantise_half(c + 1, g))
+            elif not last:
+                for g in range(PASSES):
+                    vector_extra[QUANTISE_SLOTS[g]].append(lambda g=g: quantise_half(c + 1, g))
+            if copies and c > 0:
+                for (g, b), k in zip(VECTOR_PIECES, [5, 6, 6] if c == 1 else VECTOR_SLOTS):
+                    vector_extra[k].append(lambda g=g, b=b: vector_piece(c + 2, g, b))
+            if c == CHUNKS:
+                vector_extra[6].append(lambda: add_parts(0, 0, 4))
+            if c == CHUNKS + 1:
+                vector_extra[6].append(lambda: add_parts(0, 4, ONCE))
+            if c == CHUNKS + 2:
+                vector_extra[1].append(lambda: column_means(0, 0, TILES))
+                vector_extra[4].append(lambda: row_means(0, 0, TILES))
+                vector_extra[4].append(lambda: store(0, 0, TILES))
+                gpsimd_extra[3].append(lambda: add_two_parts(1))
+            if last:
+                gpsimd_extra[0].append(lambda: add_third_part(1))
+                gpsimd_extra[FOLD_SLOT].append(early_column_means)
             done_once = 0
             done_rows = 0
             for kind, m in order:
@@ -404,36 +424,33 @@ def tile_pam_module_pa_kernel(
                 if kind == "column" and part == CHUNKS - 1:
                     pending.append(lambda m=m: sum_columns(col_sum[:, n, m, :], column_bank[m][:]))
                 if kind == "once":
+                    k = done_once
+                    done_once += 1
                     if last and m == ONCE_TILES[-1]:
-                        pending.append(lambda m=m: sum_rows(row_sum[:, n, m, ROWS * part :], once_bank[m][:]))
+                        pending = [lambda m=m: sum_rows(row_sum[:, n, m, ROWS * part :], once_bank[m][:])] + pending
                     else:
                         product = scalar_rows(c, m)
+                        if m == GPSIMD_TILE:
+                            gpsimd_product = [product]
                     for read in pending:
                         read()
                     pending = []
                     if m != GPSIMD_TILE:
                         pending.append(lambda m=m, c=c: vector_columns(c, m))
-                    if extra:
-                        extra.pop(0)()
-                    if done_once == 0:
-                        gpsimd_sum(c, product)
-                        if copies:
-                            gpsimd_piece(c + 2, 1, 2)
-                            gpsimd_piece(c + 2, 1, 3)
-                    done_once += 1
-            for step in extra:
-                step()
-            if c == 0:
+                    for step in scalar_extra[k] + vector_extra[k] + gpsimd_extra[k]:
+                        step()
+            if c == CHUNKS - 1:
                 bias_bank = banks.tile([P, P], BF16, tag="bank", name="bias_bank")
                 nc.tensor.transpose(bias_bank[:], bias_rows[:], identity[:])
                 nc.vector.tensor_copy(out=bias[:], in_=bias_bank[:, 0:TILES])
         n = BATCH - 1
-        for read in pending:
-            read()
+        for m in ONCE_TILES:
+            scalar_row_mean(n, m)
+        pending[0]()
         late_column_means(n, 0, ONCE)
-        row_means(n, 0, ONCE)
         store(n, 0, ONCE)
-        vector_rows(ALL_CHUNKS - 1, twice - 1, twice)
+        pending[1]()
         column_means(n, ONCE, TILES)
+        vector_rows(ALL_CHUNKS - 1, twice - 1, twice)
         row_means(n, ONCE, TILES)
         store(n, ONCE, TILES)

@@ -52,6 +52,7 @@ LATE_SLOTS = [[0, 1], [0, 2]]
 LATE_QUANTISE_SLOTS = [[1, 2], [1, 4]]
 FOLD_SLOT = 4
 LATE_SCALAR = [0, 1]
+VECTOR_FIRST = SHARED_TILES
 
 FLOPS = 2 * OUT_ALL * CHANNELS * BATCH * PIXELS
 
@@ -115,16 +116,18 @@ def tile_pam_module_pa_kernel(
         load_scales(Wk_scales, OUT_Q, OUT_K)
         load_words(Wq_words, 0, OUT_Q, slice(0, PASSES))
         load_words(Wk_words, OUT_Q, OUT_K, slice(0, PASSES))
-        for c in range(2, CHUNKS):
-            load_chunk(c)
+        load_chunk(2)
 
         bias_rows = keep.tile([P, P], BF16)
         nc.vector.memset(bias_rows[:], 0.0)
         nc.sync.dma_start(out=bias_rows[0:1, :], in_=bq.rearrange("(m p) -> m p", p=P))
         nc.sync.dma_start(out=bias_rows[1:2, :], in_=bk.rearrange("(m p) -> m p", p=P))
         nc.sync.dma_start(out=bias_rows[2:TILES, :], in_=bv.rearrange("(m p) -> m p", p=P))
-        for c in range(CHUNKS, ALL_CHUNKS):
+        identity = keep.tile([P, P], BF16)
+        make_identity(nc, identity[:])
+        for c in range(3, ALL_CHUNKS):
             load_chunk(c)
+
 
         grouped = {}
         x_codes = {}
@@ -339,8 +342,6 @@ def tile_pam_module_pa_kernel(
             for b in range(BLOCKS - 1):
                 vector_piece(0, g, b)
             quantise_half(0, g)
-        identity = keep.tile([P, P], BF16)
-        make_identity(nc, identity[:])
         new_grouped(1)
 
         row_steps = [("row", m) for m in TWICE_TILES]
@@ -429,20 +430,22 @@ def tile_pam_module_pa_kernel(
                     if last and m == ONCE_TILES[-1]:
                         pending = [lambda m=m: sum_rows(row_sum[:, n, m, ROWS * part :], once_bank[m][:])] + pending
                     else:
+                        if m in VECTOR_FIRST:
+                            vector_columns(c, m)
                         product = scalar_rows(c, m)
                         if m == GPSIMD_TILE:
                             gpsimd_product = [product]
                     for read in pending:
                         read()
                     pending = []
-                    if m != GPSIMD_TILE:
+                    if m != GPSIMD_TILE and (m not in VECTOR_FIRST or last and m == ONCE_TILES[-1]):
                         pending.append(lambda m=m, c=c: vector_columns(c, m))
                     for step in scalar_extra[k] + vector_extra[k] + gpsimd_extra[k]:
                         step()
-            if c == CHUNKS - 1:
-                bias_bank = banks.tile([P, P], BF16, tag="bank", name="bias_bank")
-                nc.tensor.transpose(bias_bank[:], bias_rows[:], identity[:])
-                nc.vector.tensor_copy(out=bias[:], in_=bias_bank[:, 0:TILES])
+                    if c == 2 and k == 0:
+                        bias_bank = row_banks.tile([P, P], BF16, tag="row_bank", name="bias_bank")
+                        nc.tensor.transpose(bias_bank[:], bias_rows[:], identity[:])
+                        nc.vector.tensor_copy(out=bias[:], in_=bias_bank[:, 0:TILES])
         n = BATCH - 1
         for m in ONCE_TILES:
             scalar_row_mean(n, m)

@@ -34,18 +34,18 @@ OUT_ALL = OUT_Q + OUT_K + OUT_V
 TILES = OUT_ALL // P
 
 TWICE_TILES = [7, 8, 9]
-GPSIMD_TILE = 2
-SHARED_TILES = [3, 4, 5, 6, 0, 1]
-ONCE_TILES = [GPSIMD_TILE] + SHARED_TILES
+GPSIMD_TILES = [2]
+ONCE_TILES = [2, 3, 4, 5, 6, 0, 1]
+SHARED_TILES = [m for m in ONCE_TILES if m not in GPSIMD_TILES]
 ONCE = len(ONCE_TILES)
 FREE_BANKS = 4
-VECTOR_PIECES = [(0, 0), (0, 1), (1, 0)]
-SCALAR_PIECES = [(1, 1)]
-GPSIMD_PIECES = [(0, 2), (0, 3), (1, 2), (1, 3)]
-VECTOR_SLOTS = [1, 1, 4]
-SCALAR_SLOTS = [3]
-GPSIMD_SLOTS = [0, 1, 4, 5]
-GPSIMD_ADD_SLOT = 3
+VECTOR_PIECES = [(0, 0),(0, 1),(1, 0)]
+SCALAR_PIECES = [(0, 2),(1, 1)]
+GPSIMD_PIECES = [(0, 3),(1, 2),(1, 3)]
+VECTOR_SLOTS = [1,1,4]
+SCALAR_SLOTS = [1,4]
+GPSIMD_SLOTS = [0,4,5]
+GPSIMD_ADD_SLOTS = [3]
 QUANTISE_SLOTS = [0, 3]
 USUAL_BETWEEN = [[("column", 0)], [("column", 1)], [("row", 0)], [("row", 1)], [("row", 2)], [("column", 2)]]
 LATE_SLOTS = [[0, 1], [0, 2]]
@@ -53,6 +53,7 @@ LATE_QUANTISE_SLOTS = [[1, 2], [1, 4]]
 FOLD_SLOT = 4
 LATE_SCALAR = [0, 1]
 VECTOR_FIRST = SHARED_TILES
+VECTOR_TILES = []
 
 FLOPS = 2 * OUT_ALL * CHANNELS * BATCH * PIXELS
 
@@ -172,7 +173,7 @@ def tile_pam_module_pa_kernel(
         bias = keep.tile([P, TILES], F32)
         early = keep.tile([P, ONCE, WIDTH], F32)
         map_sum = {}
-        nc.vector.memset(col_part[:, :, GPSIMD_TILE, 0 : CHUNKS - 1, :], 0.0)
+        nc.vector.memset(col_part[:, :, GPSIMD_TILES[0] : GPSIMD_TILES[-1] + 1, 0 : CHUNKS - 1, :], 0.0)
 
         def one_pass(out, c, m, g, first, width, start, stop):
             nc.tensor.matmul_mx(
@@ -238,11 +239,12 @@ def tile_pam_module_pa_kernel(
         def scalar_rows(c, m):
             n, part = divmod(c, CHUNKS)
             by_row = once_bank[m][:].rearrange("p (b r w) -> p r b w", b=BLOCKS, w=BLOCK_WIDTH)
-            if m == GPSIMD_TILE and part == 0:
-                map_sum[n] = keep.tile([P, ROWS, WIDTH], F32, name="map_sum%d" % n)
-                product = map_sum[n]
+            if m in GPSIMD_TILES and part == 0:
+                if n not in map_sum:
+                    map_sum[n] = keep.tile([P, len(GPSIMD_TILES), ROWS, WIDTH], F32, name="map_sum%d" % n)
+                product = map_sum[n][:, GPSIMD_TILES.index(m)]
             else:
-                product = products.tile([P, ROWS, WIDTH], F32, tag="product", name="product%d_%d" % (c, m))
+                product = products.tile([P, ROWS, WIDTH], F32, tag="product", name="product%d_%d" % (c, m))[:]
             for i in range(ROWS):
                 nc.scalar.activation(
                     out=product[:, i, :].rearrange("p (b w) -> p b w", w=BLOCK_WIDTH),
@@ -252,23 +254,31 @@ def tile_pam_module_pa_kernel(
                 )
             return product
 
-        def gpsimd_sum(c, product):
+        def gpsimd_add(c, m, product):
             n, part = divmod(c, CHUNKS)
-            so_far = map_sum[n]
             if part > 0:
-                nc.gpsimd.tensor_tensor(out=so_far[:], in0=so_far[:], in1=product[:], op=ADD)
-            if part == CHUNKS - 1:
-                for half in (ROWS // 2, ROWS // 4):
-                    nc.gpsimd.tensor_tensor(
-                        out=so_far[:, 0:half, :], in0=so_far[:, 0:half, :], in1=so_far[:, half : 2 * half, :], op=ADD
-                    )
+                so_far = map_sum[n][:, GPSIMD_TILES.index(m)]
+                nc.gpsimd.tensor_tensor(out=so_far, in0=so_far, in1=product, op=ADD)
+
+        def gpsimd_fold(n):
+            for half in (ROWS // 2, ROWS // 4):
                 nc.gpsimd.tensor_tensor(
-                    out=col_part[:, n, GPSIMD_TILE, CHUNKS - 1, :], in0=so_far[:, 0, :], in1=so_far[:, 1, :], op=ADD
+                    out=map_sum[n][:, :, 0:half, :], in0=map_sum[n][:, :, 0:half, :], in1=map_sum[n][:, :, half : 2 * half, :], op=ADD
                 )
+            nc.gpsimd.tensor_tensor(
+                out=col_part[:, n, GPSIMD_TILES[0] : GPSIMD_TILES[-1] + 1, CHUNKS - 1, :],
+                in0=map_sum[n][:, :, 0, :],
+                in1=map_sum[n][:, :, 1, :],
+                op=ADD,
+            )
 
         def vector_columns(c, m):
             n, part = divmod(c, CHUNKS)
             sum_columns(col_part[:, n, m, part, :], once_bank[m][:])
+
+        def vector_tile_rows(c, m):
+            n, part = divmod(c, CHUNKS)
+            sum_rows(row_sum[:, n, m, ROWS * part : ROWS * (part + 1)], once_bank[m][:])
 
         def vector_rows(c, lo, hi):
             n, part = divmod(c, CHUNKS)
@@ -364,6 +374,7 @@ def tile_pam_module_pa_kernel(
         for m in TWICE_TILES:
             column_pass(0, m, 0)
 
+        gpsimd_product = {}
         pending = []
         for c in range(ALL_CHUNKS):
             n, part = divmod(c, CHUNKS)
@@ -379,20 +390,23 @@ def tile_pam_module_pa_kernel(
                     gpsimd_extra[k].append(lambda g=g, b=b: gpsimd_piece(c + 2, g, b))
                 for (g, b), k in zip(SCALAR_PIECES, SCALAR_SLOTS):
                     scalar_extra[ONCE - 1 if c == 0 else k].append(lambda g=g, b=b: scalar_piece(c + 2, g, b))
-            gpsimd_extra[GPSIMD_ADD_SLOT].append(lambda: gpsimd_sum(c, gpsimd_product[0]))
+            for m, k in zip(GPSIMD_TILES, GPSIMD_ADD_SLOTS):
+                gpsimd_extra[k].append(lambda m=m: gpsimd_add(c, m, gpsimd_product[m]))
+            if part == CHUNKS - 1:
+                gpsimd_extra[GPSIMD_ADD_SLOTS[-1]].append(lambda: gpsimd_fold(n))
             if c < 2:
                 for g in range(PASSES):
                     if c == 0:
                         scalar_extra[LATE_SCALAR[g]].append(lambda g=g: scalar_piece(1, g, BLOCKS - 1))
-                    for b in range(BLOCKS - 1):
-                        if c == 0 or (g, b) in VECTOR_PIECES:
+                    for b in range(BLOCKS):
+                        if b < BLOCKS - 1 if c == 0 else (g, b) in VECTOR_PIECES:
                             vector_extra[LATE_SLOTS[c][g]].append(lambda g=g, b=b: vector_piece(c + 1, g, b))
                     vector_extra[LATE_QUANTISE_SLOTS[c][g]].append(lambda g=g: quantise_half(c + 1, g))
             elif not last:
                 for g in range(PASSES):
                     vector_extra[QUANTISE_SLOTS[g]].append(lambda g=g: quantise_half(c + 1, g))
             if copies and c > 0:
-                for (g, b), k in zip(VECTOR_PIECES, [5, 6, 6] if c == 1 else VECTOR_SLOTS):
+                for (g, b), k in zip(VECTOR_PIECES, [5 + g for g, b in VECTOR_PIECES] if c == 1 else VECTOR_SLOTS):
                     vector_extra[k].append(lambda g=g, b=b: vector_piece(c + 2, g, b))
             if c == CHUNKS:
                 vector_extra[6].append(lambda: add_parts(0, 0, 4))
@@ -427,18 +441,22 @@ def tile_pam_module_pa_kernel(
                 if kind == "once":
                     k = done_once
                     done_once += 1
-                    if last and m == ONCE_TILES[-1]:
+                    if last and m == ONCE_TILES[-1] and m not in VECTOR_TILES:
                         pending = [lambda m=m: sum_rows(row_sum[:, n, m, ROWS * part :], once_bank[m][:])] + pending
                     else:
                         if m in VECTOR_FIRST:
                             vector_columns(c, m)
-                        product = scalar_rows(c, m)
-                        if m == GPSIMD_TILE:
-                            gpsimd_product = [product]
+                        product = None
+                        if m in VECTOR_TILES:
+                            vector_tile_rows(c, m)
+                        else:
+                            product = scalar_rows(c, m)
+                        if m in GPSIMD_TILES:
+                            gpsimd_product[m] = product
                     for read in pending:
                         read()
                     pending = []
-                    if m != GPSIMD_TILE and (m not in VECTOR_FIRST or last and m == ONCE_TILES[-1]):
+                    if m in SHARED_TILES and (m not in VECTOR_FIRST or last and m == ONCE_TILES[-1] and m not in VECTOR_TILES):
                         pending.append(lambda m=m, c=c: vector_columns(c, m))
                     for step in scalar_extra[k] + vector_extra[k] + gpsimd_extra[k]:
                         step()

@@ -34,6 +34,7 @@ OUT_ALL = OUT_Q + OUT_K + OUT_V
 TILES = OUT_ALL // P
 
 TWICE_TILES = [7, 8, 9]
+ROW_SUMMED = [7, 8, 9]
 GPSIMD_TILES = [2]
 ONCE_TILES = [2, 3, 4, 5, 6, 0, 1]
 SHARED_TILES = [m for m in ONCE_TILES if m not in GPSIMD_TILES]
@@ -44,14 +45,14 @@ SCALAR_PIECES = [(0, 2),(1, 1)]
 GPSIMD_PIECES = [(0, 3),(1, 2),(1, 3)]
 VECTOR_SLOTS = [1,1,4]
 SCALAR_SLOTS = [1,4]
-GPSIMD_SLOTS = [0,4,5]
+GPSIMD_SLOTS = [0,1,2]
 GPSIMD_ADD_SLOTS = [3]
-QUANTISE_SLOTS = [0, 3]
+QUANTISE_SLOTS = [1, 4]
 USUAL_BETWEEN = [[("column", 0)], [("column", 1)], [("row", 0)], [("row", 1)], [("row", 2)], [("column", 2)]]
-LATE_SLOTS = [[0, 1], [0, 2]]
-LATE_QUANTISE_SLOTS = [[1, 2], [1, 4]]
+LATE_SLOTS = [[1, 2], [0, 2]]
+LATE_QUANTISE_SLOTS = [[2, 3], [1, 4]]
 FOLD_SLOT = 4
-LATE_SCALAR = [0, 1]
+LATE_SCALAR = [1, 2]
 VECTOR_FIRST = SHARED_TILES
 VECTOR_TILES = []
 
@@ -100,23 +101,23 @@ def tile_pam_module_pa_kernel(
                     in_=scale_rows[4 * quadrant : 4 * quadrant + 4].bitcast(I32),
                 )
 
-        def load_words(words, first, width, passes):
+        def load_words(words, first, start, stop):
             nc.sync.dma_start(
-                out=w_codes[:, passes, first : first + width].bitcast(I32),
-                in_=words[passes].rearrange("g p n t -> p g (n t)").bitcast(I32),
+                out=w_codes[:, :, first + start : first + stop].bitcast(I32),
+                in_=words[:, :, start:stop, :].rearrange("g p n t -> p g (n t)").bitcast(I32),
             )
 
         first_v = OUT_Q + OUT_K
         load_scales(Wv_scales, first_v, OUT_V)
-        load_words(Wv_words, first_v, OUT_V, slice(0, 1))
         load_half(0, 1)
-        load_words(Wv_words, first_v, OUT_V, slice(1, 2))
+        load_words(Wv_words, first_v, 0, OUT_V // 2)
+        load_words(Wv_words, first_v, OUT_V // 2, OUT_V)
         load_half(1, 0)
         load_scales(Wq_scales, 0, OUT_Q)
         load_half(1, 1)
         load_scales(Wk_scales, OUT_Q, OUT_K)
-        load_words(Wq_words, 0, OUT_Q, slice(0, PASSES))
-        load_words(Wk_words, OUT_Q, OUT_K, slice(0, PASSES))
+        load_words(Wq_words, 0, 0, OUT_Q)
+        load_words(Wk_words, OUT_Q, 0, OUT_K)
         load_chunk(2)
 
         bias_rows = keep.tile([P, P], BF16)
@@ -204,7 +205,7 @@ def tile_pam_module_pa_kernel(
             )
 
         def row_passes(c, m):
-            k = TWICE_TILES.index(m)
+            k = ROW_SUMMED.index(m)
             if k == 0:
                 row_bank[0] = row_banks.tile([P, CHUNK // WINDOW, WINDOW], F32, tag="row_bank", name="row_bank%d" % c)
             for g in range(PASSES):
@@ -283,7 +284,7 @@ def tile_pam_module_pa_kernel(
         def vector_rows(c, lo, hi):
             n, part = divmod(c, CHUNKS)
             nc.vector.tensor_reduce(
-                out=row_sum[:, n, TWICE_TILES[0] + lo : TWICE_TILES[0] + hi, ROWS * part : ROWS * (part + 1)],
+                out=row_sum[:, n, ROW_SUMMED[0] + lo : ROW_SUMMED[0] + hi, ROWS * part : ROWS * (part + 1)],
                 in_=row_bank[0][:, lo:hi].rearrange("p m (r w) -> p m r w", w=BLOCK_WIDTH),
                 axis=AXIS_X,
                 op=ADD,
@@ -354,27 +355,24 @@ def tile_pam_module_pa_kernel(
             quantise_half(0, g)
         new_grouped(1)
 
-        row_steps = [("row", m) for m in TWICE_TILES]
+        row_steps = [("row", m) for m in ROW_SUMMED]
         column_steps = [("column", m) for m in TWICE_TILES]
         between = USUAL_BETWEEN
         usual_order = []
         for k, m in enumerate(ONCE_TILES):
             usual_order.append(("once", m))
             if k < len(between):
-                usual_order += [(kind, TWICE_TILES[i]) for kind, i in between[k]]
+                usual_order += [(kind, (ROW_SUMMED if kind == "row" else TWICE_TILES)[i]) for kind, i in between[k]]
         ahead = ONCE_TILES[:FREE_BANKS]
         first_order = [("once", m) for m in ahead] + column_steps
         for k, m in enumerate(ONCE_TILES[FREE_BANKS:]):
-            first_order += [row_steps[k], ("once", m)]
+            first_order += row_steps[k : k + 1 if k < 2 else len(row_steps)] + [("once", m)]
         last_order = [step for step in usual_order if step != row_steps[-1] and step != column_steps[-1]]
         last_order += [column_steps[-1], row_steps[-1]]
 
+        gpsimd_product = {}
         for m in ahead:
             once_pass(0, m, 0)
-        for m in TWICE_TILES:
-            column_pass(0, m, 0)
-
-        gpsimd_product = {}
         pending = []
         for c in range(ALL_CHUNKS):
             n, part = divmod(c, CHUNKS)
@@ -423,19 +421,16 @@ def tile_pam_module_pa_kernel(
             done_once = 0
             done_rows = 0
             for kind, m in order:
-                if c == 0 and (m in ahead or kind == "column"):
-                    if kind == "once":
-                        one_pass(once_bank[m][:], c, m, 1, 0, CHUNK, False, True)
-                    else:
-                        column_pass(c, m, 1)
+                if c == 0 and m in ahead:
+                    once_pass(c, m, 1)
                 else:
                     tensor_step(c, kind, m)
                 if kind == "row":
                     done_rows += 1
-                    if last and done_rows == twice - 1:
-                        pending.append(lambda: vector_rows(c, 0, twice - 1))
-                    elif done_rows == twice and not last:
-                        pending.append(lambda: vector_rows(c, 0, twice))
+                    if last and done_rows == len(ROW_SUMMED) - 1:
+                        pending.append(lambda: vector_rows(c, 0, len(ROW_SUMMED) - 1))
+                    elif done_rows == len(ROW_SUMMED) and not last:
+                        pending.append(lambda: vector_rows(c, 0, len(ROW_SUMMED)))
                 if kind == "column" and part == CHUNKS - 1:
                     pending.append(lambda m=m: sum_columns(col_sum[:, n, m, :], column_bank[m][:]))
                 if kind == "once":
@@ -449,7 +444,7 @@ def tile_pam_module_pa_kernel(
                         product = None
                         if m in VECTOR_TILES:
                             vector_tile_rows(c, m)
-                        else:
+                        elif m not in ROW_SUMMED:
                             product = scalar_rows(c, m)
                         if m in GPSIMD_TILES:
                             gpsimd_product[m] = product
@@ -472,6 +467,6 @@ def tile_pam_module_pa_kernel(
         store(n, 0, ONCE)
         pending[1]()
         column_means(n, ONCE, TILES)
-        vector_rows(ALL_CHUNKS - 1, twice - 1, twice)
+        vector_rows(ALL_CHUNKS - 1, len(ROW_SUMMED) - 1, len(ROW_SUMMED))
         row_means(n, ONCE, TILES)
         store(n, ONCE, TILES)

@@ -40,21 +40,20 @@ ONCE_TILES = [2, 3, 4, 5, 6, 0, 1]
 SHARED_TILES = [m for m in ONCE_TILES if m not in GPSIMD_TILES]
 ONCE = len(ONCE_TILES)
 FREE_BANKS = 4
-VECTOR_PIECES = [(0, 0),(0, 1),(1, 0)]
-SCALAR_PIECES = [(0, 2),(1, 1)]
-GPSIMD_PIECES = [(0, 3),(1, 2),(1, 3)]
-VECTOR_SLOTS = [1,1,4]
+VECTOR_PIECES = [(0, 0),(1, 0)]
+SCALAR_PIECES = [(0, 1),(1, 1)]
+GPSIMD_PIECES = [(0, 2),(0, 3),(1, 2),(1, 3)]
+VECTOR_SLOTS = [1,4]
 SCALAR_SLOTS = [1,4]
-GPSIMD_SLOTS = [0,1,2]
+GPSIMD_SLOTS = [0, 1, 2, 3]
 GPSIMD_ADD_SLOTS = [3]
 QUANTISE_SLOTS = [1, 4]
 USUAL_BETWEEN = [[("column", 0)], [("column", 1)], [("row", 0)], [("row", 1)], [("row", 2)], [("column", 2)]]
 LATE_SLOTS = [[1, 2], [0, 2]]
 LATE_QUANTISE_SLOTS = [[2, 3], [1, 4]]
-FOLD_SLOT = 4
 LATE_SCALAR = [1, 2]
 VECTOR_FIRST = SHARED_TILES
-VECTOR_TILES = []
+BY_VECTOR = {0: [1], 2: [5], 4: [5], 6: [5], 7: [5, 1]}
 
 FLOPS = 2 * OUT_ALL * CHANNELS * BATCH * PIXELS
 
@@ -143,11 +142,12 @@ def tile_pam_module_pa_kernel(
             source = raw[c][:, g].rearrange("p t (r w) -> p r w t", w=WIDTH)[:, :, BLOCK_WIDTH * b : BLOCK_WIDTH * (b + 1), :]
             return target, source
 
+        def by_runs(piece):
+            return piece.rearrange("p r (v i) t -> p r v t i", i=4)
+
         def vector_piece(c, g, b):
             target, source = piece_of(c, g, b)
-            nc.vector.tensor_copy(
-                out=target.rearrange("p r (v i) t -> p r v t i", i=4), in_=source.rearrange("p r (v i) t -> p r v t i", i=4)
-            )
+            nc.vector.tensor_copy(out=by_runs(target), in_=by_runs(source))
 
         def gpsimd_piece(c, g, b):
             target, source = piece_of(c, g, b)
@@ -155,7 +155,7 @@ def tile_pam_module_pa_kernel(
 
         def scalar_piece(c, g, b):
             target, source = piece_of(c, g, b)
-            nc.scalar.copy(out=target, in_=source)
+            nc.scalar.copy(out=by_runs(target), in_=by_runs(source))
 
         def quantise_half(c, g):
             if g == 0:
@@ -366,7 +366,7 @@ def tile_pam_module_pa_kernel(
         ahead = ONCE_TILES[:FREE_BANKS]
         first_order = [("once", m) for m in ahead] + column_steps
         for k, m in enumerate(ONCE_TILES[FREE_BANKS:]):
-            first_order += row_steps[k : k + 1 if k < 2 else len(row_steps)] + [("once", m)]
+            first_order += row_steps[k : k + 1 if k < ONCE - FREE_BANKS - 1 else len(row_steps)] + [("once", m)]
         last_order = [step for step in usual_order if step != row_steps[-1] and step != column_steps[-1]]
         last_order += [column_steps[-1], row_steps[-1]]
 
@@ -404,12 +404,12 @@ def tile_pam_module_pa_kernel(
                 for g in range(PASSES):
                     vector_extra[QUANTISE_SLOTS[g]].append(lambda g=g: quantise_half(c + 1, g))
             if copies and c > 0:
-                for (g, b), k in zip(VECTOR_PIECES, [5 + g for g, b in VECTOR_PIECES] if c == 1 else VECTOR_SLOTS):
+                for (g, b), k in zip(VECTOR_PIECES, [ONCE - 2 + g for g, b in VECTOR_PIECES] if c == 1 else VECTOR_SLOTS):
                     vector_extra[k].append(lambda g=g, b=b: vector_piece(c + 2, g, b))
             if c == CHUNKS:
-                vector_extra[6].append(lambda: add_parts(0, 0, 4))
+                vector_extra[ONCE - 1].append(lambda: add_parts(0, 0, 4))
             if c == CHUNKS + 1:
-                vector_extra[6].append(lambda: add_parts(0, 4, ONCE))
+                vector_extra[ONCE - 1].append(lambda: add_parts(0, 4, ONCE))
             if c == CHUNKS + 2:
                 vector_extra[1].append(lambda: column_means(0, 0, TILES))
                 vector_extra[4].append(lambda: row_means(0, 0, TILES))
@@ -417,7 +417,7 @@ def tile_pam_module_pa_kernel(
                 gpsimd_extra[3].append(lambda: add_two_parts(1))
             if last:
                 gpsimd_extra[0].append(lambda: add_third_part(1))
-                gpsimd_extra[FOLD_SLOT].append(early_column_means)
+                gpsimd_extra[0].append(early_column_means)
             done_once = 0
             done_rows = 0
             for kind, m in order:
@@ -436,22 +436,20 @@ def tile_pam_module_pa_kernel(
                 if kind == "once":
                     k = done_once
                     done_once += 1
-                    if last and m == ONCE_TILES[-1] and m not in VECTOR_TILES:
-                        pending = [lambda m=m: sum_rows(row_sum[:, n, m, ROWS * part :], once_bank[m][:])] + pending
-                    else:
+                    product = None
+                    if m not in ROW_SUMMED and m not in BY_VECTOR.get(c, []):
                         if m in VECTOR_FIRST:
                             vector_columns(c, m)
-                        product = None
-                        if m in VECTOR_TILES:
-                            vector_tile_rows(c, m)
-                        elif m not in ROW_SUMMED:
-                            product = scalar_rows(c, m)
-                        if m in GPSIMD_TILES:
-                            gpsimd_product[m] = product
+                        product = scalar_rows(c, m)
+                    if m in GPSIMD_TILES:
+                        gpsimd_product[m] = product
                     for read in pending:
                         read()
                     pending = []
-                    if m in SHARED_TILES and (m not in VECTOR_FIRST or last and m == ONCE_TILES[-1] and m not in VECTOR_TILES):
+                    if m in BY_VECTOR.get(c, []):
+                        vector_tile_rows(c, m)
+                        vector_columns(c, m)
+                    elif m in SHARED_TILES and m not in VECTOR_FIRST:
                         pending.append(lambda m=m, c=c: vector_columns(c, m))
                     for step in scalar_extra[k] + vector_extra[k] + gpsimd_extra[k]:
                         step()
@@ -462,10 +460,10 @@ def tile_pam_module_pa_kernel(
         n = BATCH - 1
         for m in ONCE_TILES:
             scalar_row_mean(n, m)
-        pending[0]()
         late_column_means(n, 0, ONCE)
         store(n, 0, ONCE)
-        pending[1]()
+        for read in pending:
+            read()
         column_means(n, ONCE, TILES)
         vector_rows(ALL_CHUNKS - 1, len(ROW_SUMMED) - 1, len(ROW_SUMMED))
         row_means(n, ONCE, TILES)

from contextlib import ExitStack

import concourse.mybir as mybir
from concourse.masks import make_identity

F32 = mybir.dt.float32
BF16 = mybir.dt.bfloat16
U8 = mybir.dt.uint8
U32 = mybir.dt.uint32
I32 = mybir.dt.int32
FP8X4 = mybir.dt.float8_e4m3fn_x4
ADD = mybir.AluOpType.add
MULT = mybir.AluOpType.mult
AXIS_X = mybir.AxisListType.X
AXIS_XY = mybir.AxisListType.XY
COPY = mybir.ActivationFunctionType.Copy
IDENTITY = mybir.ActivationFunctionType.Identity

P = 128
PACK = 4
K_PASS = P * PACK
BATCH, CHANNELS, HEIGHT, WIDTH = 2, 1024, 32, 64
PASSES = CHANNELS // K_PASS
PIXELS = HEIGHT * WIDTH
CHUNK = 512
ROWS = CHUNK // WIDTH
CHUNKS = PIXELS // CHUNK
ALL_CHUNKS = BATCH * CHUNKS
BLOCKS = 4
BLOCK_WIDTH = WIDTH // BLOCKS
WINDOW = ROWS * BLOCK_WIDTH
OUT_Q, OUT_K, OUT_V = 128, 128, 1024
OUT_ALL = OUT_Q + OUT_K + OUT_V
TILES = OUT_ALL // P

TWICE_TILES = [7, 8, 9]
ROW_SUMMED = [7, 8, 9]
GPSIMD_TILES = [2]
ONCE_TILES = [2, 3, 4, 5, 6, 0, 1]
SHARED_TILES = [m for m in ONCE_TILES if m not in GPSIMD_TILES]
ONCE = len(ONCE_TILES)
FREE_BANKS = 4
VECTOR_PIECES = [(0, 0),(1, 0)]
SCALAR_PIECES = [(0, 1),(1, 1)]
GPSIMD_PIECES = [(0, 2),(0, 3),(1, 2),(1, 3)]
VECTOR_SLOTS = [1,4]
SCALAR_SLOTS = [1,4]
GPSIMD_SLOTS = [0, 1, 2, 3]
GPSIMD_ADD_SLOTS = [3]
QUANTISE_SLOTS = [1, 4]
USUAL_BETWEEN = [[("column", 0)], [("column", 1)], [("row", 0)], [("row", 1)], [("row", 2)], [("column", 2)]]
LATE_SLOTS = [[1, 2], [0, 2]]
LATE_QUANTISE_SLOTS = [[2, 3], [1, 4]]
LATE_SCALAR = [1, 2]
VECTOR_FIRST = SHARED_TILES
BY_VECTOR = {0: [1], 2: [5], 4: [5], 6: [5], 7: [5, 1]}

FLOPS = 2 * OUT_ALL * CHANNELS * BATCH * PIXELS


def tile_pam_module_pa_kernel(
    tc, x, Wq_words, Wq_scales, bq, Wk_words, Wk_scales, bk, Wv_words, Wv_scales, bv, out_0, out_1, out_2
):
    nc = tc.nc
    twice = len(TWICE_TILES)

    with ExitStack() as ctx:
        keep = ctx.enter_context(tc.tile_pool(name="keep", bufs=1))
        stage = ctx.enter_context(tc.tile_pool(name="stage", bufs=3))
        products = ctx.enter_context(tc.tile_pool(name="products", bufs=6))
        banks = ctx.enter_context(tc.psum_pool(name="banks", bufs=FREE_BANKS))
        row_banks = ctx.enter_context(tc.psum_pool(name="row_banks", bufs=1))
        column_banks = ctx.enter_context(tc.psum_pool(name="column_banks", bufs=twice))
        ctx.enter_context(tc.manual_schedule())

        x_view = x.rearrange("n (g p t) h w -> n g p t (h w)", g=PASSES, p=P, t=PACK)
        raw = {}

        def load_half(c, g):
            n, part = divmod(c, CHUNKS)
            if g == 0:
                raw[c] = keep.tile([P, PASSES, PACK, CHUNK], BF16, name="raw%d" % c)
            nc.sync.dma_start(out=raw[c][:, g], in_=x_view[n, g, :, :, CHUNK * part : CHUNK * (part + 1)])

        def load_chunk(c):
            for g in range(PASSES):
                load_half(c, g)

        load_half(0, 0)

        w_codes = keep.tile([P, PASSES, OUT_ALL], U32, align_bytes=64)
        w_scales = keep.tile([P, PASSES, OUT_ALL], U8, align_bytes=64)
        nc.vector.memset(w_scales[:].bitcast(I32), 0)

        def load_scales(scales, first, width):
            scale_rows = scales.rearrange("g q n -> q g n")
            for quadrant in range(4):
                nc.sync.dma_start(
                    out=w_scales[32 * quadrant : 32 * quadrant + 4, :, first : first + width].bitcast(I32),
                    in_=scale_rows[4 * quadrant : 4 * quadrant + 4].bitcast(I32),
                )

        def load_words(words, first, start, stop):
            nc.sync.dma_start(
                out=w_codes[:, :, first + start : first + stop].bitcast(I32),
                in_=words[:, :, start:stop, :].rearrange("g p n t -> p g (n t)").bitcast(I32),
            )

        first_v = OUT_Q + OUT_K
        load_scales(Wv_scales, first_v, OUT_V)
        load_half(0, 1)
        load_words(Wv_words, first_v, 0, OUT_V // 2)
        load_words(Wv_words, first_v, OUT_V // 2, OUT_V)
        load_half(1, 0)
        load_scales(Wq_scales, 0, OUT_Q)
        load_half(1, 1)
        load_scales(Wk_scales, OUT_Q, OUT_K)
        load_words(Wq_words, 0, 0, OUT_Q)
        load_words(Wk_words, OUT_Q, 0, OUT_K)
        load_chunk(2)

        bias_rows = keep.tile([P, P], BF16)
        nc.vector.memset(bias_rows[:], 0.0)
        nc.sync.dma_start(out=bias_rows[0:1, :], in_=bq.rearrange("(m p) -> m p", p=P))
        nc.sync.dma_start(out=bias_rows[1:2, :], in_=bk.rearrange("(m p) -> m p", p=P))
        nc.sync.dma_start(out=bias_rows[2:TILES, :], in_=bv.rearrange("(m p) -> m p", p=P))
        identity = keep.tile([P, P], BF16)
        make_identity(nc, identity[:])
        for c in range(3, ALL_CHUNKS):
            load_chunk(c)


        grouped = {}
        x_codes = {}
        x_scales = {}

        def new_grouped(c):
            grouped[c] = stage.tile([P, PASSES, CHUNK, PACK], BF16, tag="grouped", name="grouped%d" % c, align_bytes=64)

        def piece_of(c, g, b):
            target = grouped[c][:, g, WINDOW * b : WINDOW * (b + 1), :].rearrange("p (r w) t -> p r w t", w=BLOCK_WIDTH)
            source = raw[c][:, g].rearrange("p t (r w) -> p r w t", w=WIDTH)[:, :, BLOCK_WIDTH * b : BLOCK_WIDTH * (b + 1), :]
            return target, source

        def by_runs(piece):
            return piece.rearrange("p r (v i) t -> p r v t i", i=4)

        def vector_piece(c, g, b):
            target, source = piece_of(c, g, b)
            nc.vector.tensor_copy(out=by_runs(target), in_=by_runs(source))

        def gpsimd_piece(c, g, b):
            target, source = piece_of(c, g, b)
            nc.gpsimd.tensor_scalar(out=target, in0=source, scalar1=1.0, scalar2=0.0, op0=MULT, op1=ADD)

        def scalar_piece(c, g, b):
            target, source = piece_of(c, g, b)
            nc.scalar.copy(out=by_runs(target), in_=by_runs(source))

        def quantise_half(c, g):
            if g == 0:
                x_codes[c] = keep.tile([P, PASSES, CHUNK], U32, name="x_codes%d" % c, align_bytes=64)
                x_scales[c] = keep.tile([P, PASSES, CHUNK], U8, name="x_scales%d" % c, align_bytes=64)
            nc.vector.quantize_mx(
                out=x_codes[c][:, g].bitcast(FP8X4),
                scales=x_scales[c][:, g],
                in_=grouped[c][:, g].rearrange("p w t -> p (w t)"),
            )

        row_sum = keep.tile([P, BATCH, TILES, HEIGHT], F32)
        col_part = keep.tile([P, BATCH, ONCE, CHUNKS, WIDTH], F32)
        col_sum = keep.tile([P, BATCH, TILES, WIDTH], F32)
        pooled = keep.tile([P, BATCH, TILES, HEIGHT + WIDTH], F32)
        bias = keep.tile([P, TILES], F32)
        early = keep.tile([P, ONCE, WIDTH], F32)
        map_sum = {}
        nc.vector.memset(col_part[:, :, GPSIMD_TILES[0] : GPSIMD_TILES[-1] + 1, 0 : CHUNKS - 1, :], 0.0)

        def one_pass(out, c, m, g, first, width, start, stop):
            nc.tensor.matmul_mx(
                out=out,
                lhsT=w_codes[:, g, P * m : P * (m + 1)].bitcast(FP8X4),
                lhsT_scale=w_scales[:, g, P * m : P * (m + 1)],
                rhs=x_codes[c][:, g, first : first + width].bitcast(FP8X4),
                rhs_scale=x_scales[c][:, g, first : first + width],
                start=start,
                stop=stop,
            )

        once_bank = {}
        row_bank = {}
        column_bank = {}

        def once_pass(c, m, g):
            if g == 0:
                once_bank[m] = banks.tile([P, CHUNK], F32, tag="bank", name="bank%d_%d" % (c, m))
            one_pass(once_bank[m][:], c, m, g, 0, CHUNK, g == 0, g == PASSES - 1)

        def column_pass(c, m, g):
            part = c % CHUNKS
            if part == 0 and g == 0:
                column_bank[m] = column_banks.tile([P, CHUNK], F32, tag="column_bank", name="column_bank%d_%d" % (c, m))
            one_pass(
                column_bank[m][:], c, m, g, 0, CHUNK, part == 0 and g == 0, part == CHUNKS - 1 and g == PASSES - 1
            )

        def row_passes(c, m):
            k = ROW_SUMMED.index(m)
            if k == 0:
                row_bank[0] = row_banks.tile([P, CHUNK // WINDOW, WINDOW], F32, tag="row_bank", name="row_bank%d" % c)
            for g in range(PASSES):
                for b in range(BLOCKS):
                    one_pass(
                        row_bank[0][:, k], c, m, g, WINDOW * b, WINDOW, g == 0 and b == 0, g == PASSES - 1 and b == BLOCKS - 1
                    )

        def tensor_step(c, kind, m):
            if kind == "row":
                row_passes(c, m)
                return
            for g in range(PASSES):
                if kind == "once":
                    once_pass(c, m, g)
                else:
                    column_pass(c, m, g)

        def sum_columns(out, bank):
            nc.vector.tensor_reduce(
                out=out.rearrange("p (b w) -> p b w", w=BLOCK_WIDTH),
                in_=bank.rearrange("p (b r w) -> p b w r", b=BLOCKS, w=BLOCK_WIDTH),
                axis=AXIS_X,
                op=ADD,
            )

        def sum_rows(out, bank):
            nc.vector.tensor_reduce(
                out=out, in_=bank.rearrange("p (b r w) -> p r b w", b=BLOCKS, w=BLOCK_WIDTH), axis=AXIS_XY, op=ADD
            )

        def scalar_rows(c, m):
            n, part = divmod(c, CHUNKS)
            by_row = once_bank[m][:].rearrange("p (b r w) -> p r b w", b=BLOCKS, w=BLOCK_WIDTH)
            if m in GPSIMD_TILES and part == 0:
                if n not in map_sum:
                    map_sum[n] = keep.tile([P, len(GPSIMD_TILES), ROWS, WIDTH], F32, name="map_sum%d" % n)
                product = map_sum[n][:, GPSIMD_TILES.index(m)]
            else:
                product = products.tile([P, ROWS, WIDTH], F32, tag="product", name="product%d_%d" % (c, m))[:]
            for i in range(ROWS):
                nc.scalar.activation(
                    out=product[:, i, :].rearrange("p (b w) -> p b w", w=BLOCK_WIDTH),
                    in_=by_row[:, i],
                    func=COPY,
                    accum_out=row_sum[:, n, m, ROWS * part + i : ROWS * part + i + 1],
                )
            return product

        def gpsimd_add(c, m, product):
            n, part = divmod(c, CHUNKS)
            if part > 0:
                so_far = map_sum[n][:, GPSIMD_TILES.index(m)]
                nc.gpsimd.tensor_tensor(out=so_far, in0=so_far, in1=product, op=ADD)

        def gpsimd_fold(n):
            for half in (ROWS // 2, ROWS // 4):
                nc.gpsimd.tensor_tensor(
                    out=map_sum[n][:, :, 0:half, :], in0=map_sum[n][:, :, 0:half, :], in1=map_sum[n][:, :, half : 2 * half, :], op=ADD
                )
            nc.gpsimd.tensor_tensor(
                out=col_part[:, n, GPSIMD_TILES[0] : GPSIMD_TILES[-1] + 1, CHUNKS - 1, :],
                in0=map_sum[n][:, :, 0, :],
                in1=map_sum[n][:, :, 1, :],
                op=ADD,
            )

        def vector_columns(c, m):
            n, part = divmod(c, CHUNKS)
            sum_columns(col_part[:, n, m, part, :], once_bank[m][:])

        def vector_tile_rows(c, m):
            n, part = divmod(c, CHUNKS)
            sum_rows(row_sum[:, n, m, ROWS * part : ROWS * (part + 1)], once_bank[m][:])

        def vector_rows(c, lo, hi):
            n, part = divmod(c, CHUNKS)
            nc.vector.tensor_reduce(
                out=row_sum[:, n, ROW_SUMMED[0] + lo : ROW_SUMMED[0] + hi, ROWS * part : ROWS * (part + 1)],
                in_=row_bank[0][:, lo:hi].rearrange("p m (r w) -> p m r w", w=BLOCK_WIDTH),
                axis=AXIS_X,
                op=ADD,
            )

        def add_parts(n, lo, hi):
            nc.vector.tensor_reduce(
                out=col_sum[:, n, lo:hi, :], in_=col_part[:, n, lo:hi].rearrange("p m c j -> p m j c"), axis=AXIS_X, op=ADD
            )

        def add_two_parts(n):
            nc.gpsimd.tensor_tensor(out=early[:], in0=col_part[:, n, :, 0, :], in1=col_part[:, n, :, 1, :], op=ADD)

        def add_third_part(n):
            nc.gpsimd.tensor_tensor(out=early[:], in0=early[:], in1=col_part[:, n, :, 2, :], op=ADD)

        def early_column_means():
            for m in range(ONCE):
                nc.gpsimd.tensor_scalar(
                    out=early[:, m, :], in0=early[:, m, :], scalar1=1.0 / HEIGHT, scalar2=bias[:, m : m + 1], op0=MULT, op1=ADD
                )

        def late_column_means(n, lo, hi):
            nc.vector.scalar_tensor_tensor(
                out=pooled[:, n, lo:hi, HEIGHT:],
                in0=col_part[:, n, lo:hi, CHUNKS - 1, :],
                scalar=1.0 / HEIGHT,
                in1=early[:, lo:hi, :],
                op0=MULT,
                op1=ADD,
            )

        def mean(out, sums, lo, hi, length, count):
            nc.vector.scalar_tensor_tensor(
                out=out,
                in0=sums,
                scalar=1.0 / count,
                in1=bias[:, lo:hi].unsqueeze(2).to_broadcast([P, hi - lo, length]),
                op0=MULT,
                op1=ADD,
            )

        def scalar_row_mean(n, m):
            nc.scalar.activation(
                out=pooled[:, n, m, 0:HEIGHT], in_=row_sum[:, n, m, :], func=IDENTITY, scale=1.0 / WIDTH, bias=bias[:, m : m + 1]
            )

        def row_means(n, lo, hi):
            mean(pooled[:, n, lo:hi, 0:HEIGHT], row_sum[:, n, lo:hi, :], lo, hi, HEIGHT, WIDTH)

        def column_means(n, lo, hi):
            mean(pooled[:, n, lo:hi, HEIGHT:], col_sum[:, n, lo:hi, :], lo, hi, WIDTH, HEIGHT)

        def store(n, lo, hi):
            if lo == 0:
                nc.sync.dma_start(out=out_0[n], in_=pooled[:, n, 0, :])
                nc.sync.dma_start(out=out_1[n], in_=pooled[:, n, 1, :])
            first = max(lo, 2)
            nc.sync.dma_start(
                out=out_2[n].rearrange("(m p) f -> p m f", p=P)[:, first - 2 : hi - 2, :], in_=pooled[:, n, first:hi, :]
            )

        new_grouped(0)
        for g in range(PASSES):
            scalar_piece(0, g, BLOCKS - 1)
            for b in range(BLOCKS - 1):
                vector_piece(0, g, b)
            quantise_half(0, g)
        new_grouped(1)

        row_steps = [("row", m) for m in ROW_SUMMED]
        column_steps = [("column", m) for m in TWICE_TILES]
        between = USUAL_BETWEEN
        usual_order = []
        for k, m in enumerate(ONCE_TILES):
            usual_order.append(("once", m))
            if k < len(between):
                usual_order += [(kind, (ROW_SUMMED if kind == "row" else TWICE_TILES)[i]) for kind, i in between[k]]
        ahead = ONCE_TILES[:FREE_BANKS]
        first_order = [("once", m) for m in ahead] + column_steps
        for k, m in enumerate(ONCE_TILES[FREE_BANKS:]):
            first_order += row_steps[k : k + 1 if k < ONCE - FREE_BANKS - 1 else len(row_steps)] + [("once", m)]
        last_order = [step for step in usual_order if step != row_steps[-1] and step != column_steps[-1]]
        last_order += [column_steps[-1], row_steps[-1]]

        gpsimd_product = {}
        for m in ahead:
            once_pass(0, m, 0)
        pending = []
        for c in range(ALL_CHUNKS):
            n, part = divmod(c, CHUNKS)
            last = c == ALL_CHUNKS - 1
            order = first_order if c == 0 else last_order if last else usual_order
            copies = c + 2 < ALL_CHUNKS
            vector_extra = [[] for k in range(ONCE)]
            scalar_extra = [[] for k in range(ONCE)]
            gpsimd_extra = [[] for k in range(ONCE)]
            if copies:
                new_grouped(c + 2)
                for (g, b), k in zip(GPSIMD_PIECES, GPSIMD_SLOTS):
                    gpsimd_extra[k].append(lambda g=g, b=b: gpsimd_piece(c + 2, g, b))
                for (g, b), k in zip(SCALAR_PIECES, SCALAR_SLOTS):
                    scalar_extra[ONCE - 1 if c == 0 else k].append(lambda g=g, b=b: scalar_piece(c + 2, g, b))
            for m, k in zip(GPSIMD_TILES, GPSIMD_ADD_SLOTS):
                gpsimd_extra[k].append(lambda m=m: gpsimd_add(c, m, gpsimd_product[m]))
            if part == CHUNKS - 1:
                gpsimd_extra[GPSIMD_ADD_SLOTS[-1]].append(lambda: gpsimd_fold(n))
            if c < 2:
                for g in range(PASSES):
                    if c == 0:
                        scalar_extra[LATE_SCALAR[g]].append(lambda g=g: scalar_piece(1, g, BLOCKS - 1))
                    for b in range(BLOCKS):
                        if b < BLOCKS - 1 if c == 0 else (g, b) in VECTOR_PIECES:
                            vector_extra[LATE_SLOTS[c][g]].append(lambda g=g, b=b: vector_piece(c + 1, g, b))
                    vector_extra[LATE_QUANTISE_SLOTS[c][g]].append(lambda g=g: quantise_half(c + 1, g))
            elif not last:
                for g in range(PASSES):
                    vector_extra[QUANTISE_SLOTS[g]].append(lambda g=g: quantise_half(c + 1, g))
            if copies and c > 0:
                for (g, b), k in zip(VECTOR_PIECES, [ONCE - 2 + g for g, b in VECTOR_PIECES] if c == 1 else VECTOR_SLOTS):
                    vector_extra[k].append(lambda g=g, b=b: vector_piece(c + 2, g, b))
            if c == CHUNKS:
                vector_extra[ONCE - 1].append(lambda: add_parts(0, 0, 4))
            if c == CHUNKS + 1:
                vector_extra[ONCE - 1].append(lambda: add_parts(0, 4, ONCE))
            if c == CHUNKS + 2:
                vector_extra[1].append(lambda: column_means(0, 0, TILES))
                vector_extra[4].append(lambda: row_means(0, 0, TILES))
                vector_extra[4].append(lambda: store(0, 0, TILES))
                gpsimd_extra[3].append(lambda: add_two_parts(1))
            if last:
                gpsimd_extra[0].append(lambda: add_third_part(1))
                gpsimd_extra[0].append(early_column_means)
            done_once = 0
            done_rows = 0
            for kind, m in order:
                if c == 0 and m in ahead:
                    once_pass(c, m, 1)
                else:
                    tensor_step(c, kind, m)
                if kind == "row":
                    done_rows += 1
                    if last and done_rows == len(ROW_SUMMED) - 1:
                        pending.append(lambda: vector_rows(c, 0, len(ROW_SUMMED) - 1))
                    elif done_rows == len(ROW_SUMMED) and not last:
                        pending.append(lambda: vector_rows(c, 0, len(ROW_SUMMED)))
                if kind == "column" and part == CHUNKS - 1:
                    pending.append(lambda m=m: sum_columns(col_sum[:, n, m, :], column_bank[m][:]))
                if kind == "once":
                    k = done_once
                    done_once += 1
                    product = None
                    if m not in ROW_SUMMED and m not in BY_VECTOR.get(c, []):
                        if m in VECTOR_FIRST:
                            vector_columns(c, m)
                        product = scalar_rows(c, m)
                    if m in GPSIMD_TILES:
                        gpsimd_product[m] = product
                    for read in pending:
                        read()
                    pending = []
                    if m in BY_VECTOR.get(c, []):
                        vector_tile_rows(c, m)
                        vector_columns(c, m)
                    elif m in SHARED_TILES and m not in VECTOR_FIRST:
                        pending.append(lambda m=m, c=c: vector_columns(c, m))
                    for step in scalar_extra[k] + vector_extra[k] + gpsimd_extra[k]:
                        step()
                    if c == 2 and k == 0:
                        bias_bank = row_banks.tile([P, P], BF16, tag="row_bank", name="bias_bank")
                        nc.tensor.transpose(bias_bank[:], bias_rows[:], identity[:])
                        nc.vector.tensor_copy(out=bias[:], in_=bias_bank[:, 0:TILES])
        n = BATCH - 1
        for m in ONCE_TILES:
            scalar_row_mean(n, m)
        late_column_means(n, 0, ONCE)
        store(n, 0, ONCE)
        for read in pending:
            read()
        column_means(n, ONCE, TILES)
        vector_rows(ALL_CHUNKS - 1, len(ROW_SUMMED) - 1, len(ROW_SUMMED))
        row_means(n, ONCE, TILES)
        store(n, ONCE, TILES)
